import numpy as np
import ml_dtypes


def mxq(x, axis, fmt="e4m3"):
    dtype, down = {"e4m3": (ml_dtypes.float8_e4m3fn, 7), "e5m2": (ml_dtypes.float8_e5m2, 14)}[fmt]
    v = np.moveaxis(np.asarray(x, np.float32).astype(ml_dtypes.bfloat16).astype(np.float64), axis, -1)
    blocks = v.reshape(v.shape[:-1] + (-1, 32))
    amax = np.abs(blocks).max(-1, keepdims=True)
    byte = np.maximum(np.where(amax > 0, np.frexp(amax)[1] - 1 + 127, 0) - down, 1)
    scale = np.exp2(byte - 127.0)
    codes = (blocks / scale).astype(np.float32).astype(dtype).astype(np.float64)
    return np.moveaxis((codes * scale).reshape(v.shape), -1, axis)


WIDE = False


def mx_kscale(k):
    if not WIDE:
        return np.ones(k)
    levels = np.array([10, -10, 5, -5, 0])
    a = np.random.permutation(np.resize(levels, k // 512 * 4)).reshape(k // 512, 4)
    idx = np.arange(k)
    return np.exp2(a[idx // 512, idx % 128 // 32])


BF16 = ml_dtypes.bfloat16


def bf(x):
    return np.asarray(x, np.float32).astype(BF16)


def f64(x):
    return np.asarray(x).astype(np.float64)


E2M1 = np.array([0.0, 0.5, 1.0, 1.5, 2.0, 3.0, 4.0, 6.0, -0.0, -0.5, -1.0, -1.5, -2.0, -3.0, -4.0, -6.0])


def pack_weight(w, fmt):
    k, n = w.shape
    w = f64(bf(w)).reshape(k // 32, 32, n)
    amax = np.abs(w).max(1)
    if fmt == "e4m3":
        byte = np.frexp(amax)[1] - 1 + 127 - 7
    else:
        mant, ex = np.frexp(amax / 6.0)
        byte = np.where(mant > 0.5, ex, ex - 1) + 127
    byte = np.clip(np.where(amax > 0, byte, 1), 1, 254)
    scaled = (w * np.exp2(127.0 - byte)[:, None, :]).reshape(k, n).astype(np.float32)
    by_word = np.ascontiguousarray(scaled.reshape(k // 512, 128, 4, n).transpose(0, 1, 3, 2))
    if fmt == "e4m3":
        words = by_word.astype(ml_dtypes.float8_e4m3fn).view(np.uint8)
    else:
        c = by_word.astype(ml_dtypes.float4_e2m1fn).view(np.uint8) & 0xF
        words = c[..., 0::2] | (c[..., 1::2] << 4)
    return np.ascontiguousarray(words), np.ascontiguousarray(byte.astype(np.uint8).reshape(k // 512, 16, n))


def unpack_weight(words, scales, fmt):
    g, p, n, _ = words.shape
    if fmt == "e4m3":
        vals = np.ascontiguousarray(words).view(ml_dtypes.float8_e4m3fn).astype(np.float64)
    else:
        nib = np.empty((g, p, n, 4), np.uint8)
        nib[..., 0::2] = words & 0xF
        nib[..., 1::2] = words >> 4
        vals = E2M1[nib]
    vals = vals * np.repeat(np.exp2(scales.astype(np.float64) - 127.0), 8, axis=1)[..., None]
    return vals.transpose(0, 1, 3, 2).reshape(g * 512, n)


B, I, O, G, P = 128, 1024, 2048, 5, 3
GRID_RANGE = (-1.0, 1.0)
L = G + P


def make_grid():
    h = (GRID_RANGE[1] - GRID_RANGE[0]) / G
    n = G + 2 * P + 1
    return np.linspace(GRID_RANGE[0] - P * h, GRID_RANGE[1] + P * h, n)


def b_spline(x, grid, k):
    x = x[..., None]
    g = grid[None, None, :]
    basis = ((x >= g[..., :-1]) & (x < g[..., 1:])).astype(np.float64)
    for p in range(1, k + 1):
        left_denom = g[..., p:-1] - g[..., :-(p + 1)]
        right_denom = g[..., p + 1:] - g[..., 1:-p]
        left_denom = np.where(left_denom > 0, left_denom, np.ones_like(left_denom))
        right_denom = np.where(right_denom > 0, right_denom, np.ones_like(right_denom))
        left = (x - g[..., :-(p + 1)]) / left_denom * basis[..., :-1]
        right = (g[..., p + 1:] - x) / right_denom * basis[..., 1:]
        basis = left + right
    return basis


def setup_inputs():
    s = mx_kscale(I)
    s = s / s.max()
    x = bf(np.random.uniform(-1.0, 1.0, (B, I)) * s)
    base_weight = np.random.uniform(-1.0, 1.0, (O, I)) * 3.0 / np.sqrt(I) / s
    base_weight_words, base_weight_scales = pack_weight(np.ascontiguousarray(base_weight.T), "e4m3")
    spline_weight = bf(np.random.standard_normal((O, I, L)) * 1.5 / np.sqrt(I))
    return {"x": x,
            "base_weight_words": base_weight_words,
            "base_weight_scales": base_weight_scales,
            "spline_weight": spline_weight}


def reference(x, base_weight_words, base_weight_scales, spline_weight):
    x = f64(x)
    grid = make_grid()
    scale_base, scale_spline = 1.0, 1.0
    base_out = mxq(x, 1, "e4m3") @ unpack_weight(base_weight_words, base_weight_scales, "e4m3")
    basis = b_spline(x, grid, P)
    spline_out = mxq(basis.reshape(B, I * L), 1, "e4m3") @ mxq(f64(spline_weight).reshape(O, I * L), 1, "e4m3").T
    return scale_base * base_out + scale_spline * spline_out

@@ -1,0 +1,209 @@
+from contextlib import ExitStack
+import math
+
+from concourse import mybir
+from concourse.masks import make_identity
+
+F32 = mybir.dt.float32
+BF16 = mybir.dt.bfloat16
+U32 = mybir.dt.uint32
+U8 = mybir.dt.uint8
+I32 = mybir.dt.int32
+FP8X4 = mybir.dt.float8_e4m3fn_x4
+ACT = mybir.ActivationFunctionType
+ALU = mybir.AluOpType
+AX = mybir.AxisListType
+
+P = 128
+B, I, O, L = 128, 1024, 2048, 8
+K = I * L
+FLOPS = 2 * B * (I + K) * O
+N_TILE = 512
+KC = 2048
+PASSES_U = KC // 512
+N_OQ = O // N_TILE
+N_KC = K // KC
+VEC_BANKS = (3,)
+
+
+def tile_kanlayer_w_kernel(tc, x, base_weight_words, base_weight_scales, spline_weight, out):
+    nc = tc.nc
+    w2 = spline_weight.rearrange("o i l -> o (i l)")
+    with ExitStack() as ctx:
+        const = ctx.enter_context(tc.tile_pool(name="const", bufs=1))
+        wpool = ctx.enter_context(tc.tile_pool(name="wraw", bufs=4))
+        gpool = ctx.enter_context(tc.tile_pool(name="grp", bufs=6))
+        cpool = ctx.enter_context(tc.tile_pool(name="codes", bufs=8))
+        bpool = ctx.enter_context(tc.tile_pool(name="basis", bufs=2))
+        opool = ctx.enter_context(tc.tile_pool(name="outs", bufs=2))
+        accp = ctx.enter_context(tc.psum_pool(name="acc", bufs=1))
+        tpp = ctx.enter_context(tc.psum_pool(name="tp", bufs=4))
+
+        x_sb = const.tile([P, I], BF16, align_bytes=64)
+        nc.sync.dma_start(out=x_sb[:], in_=x)
+        planes = const.tile([P, 2, O], U8, align_bytes=64)
+        nc.vector.memset(planes[:].rearrange("p g n -> p (g n)").bitcast(I32), 0)
+        for q in range(4):
+            nc.sync.dma_start(
+                out=planes[32 * q:32 * q + 4, :, :].bitcast(I32),
+                in_=base_weight_scales[:, 4 * q:4 * q + 4, :].rearrange("g r n -> r g n").bitcast(I32),
+            )
+
+        ident_f = const.tile([P, P], F32)
+        make_identity(nc, ident_f[:])
+        ident_b = const.tile([P, P], BF16)
+        nc.vector.tensor_copy(out=ident_b[:], in_=ident_f[:])
+        lrow = const.tile([P, 32, 4], F32)
+        for r in range(4):
+            nc.vector.memset(lrow[:, :, r], 3.5 - 2.0 * r)
+        lsel = const.tile([P, P], F32)
+        nc.vector.tensor_tensor(out=lsel[:], in0=ident_f[:], in1=lrow[:].rearrange("p a r -> p (a r)"), op=ALU.mult)
+        cb = const.tile([P, 2], F32)
+        nc.vector.tensor_reduce(out=cb[:, 0:1], in_=lsel[:], axis=AX.X, op=ALU.add)
+        nc.vector.tensor_scalar_add(out=cb[:, 1:2], in0=cb[:, 0:1], scalar1=-1.0)
+
+        bcodes = const.tile([P, K // 512, B], U32, align_bytes=64)
+        bscl = const.tile([P, K // 512, B], U8, align_bytes=64)
+        xcodes = const.tile([P, 2, B], U32, align_bytes=64)
+        xscl = const.tile([P, 2, B], U8, align_bytes=64)
+        bw = const.tile([P, 2, O], U32, align_bytes=64)
+
+        acc = [accp.tile([P, N_TILE], F32, name="acc%d" % q) for q in range(N_OQ)]
+
+        def load_unit(kc, oq):
+            wraw = wpool.tile([P, 4, KC], BF16, tag="wraw", name="wraw")
+            nc.sync.dma_start(
+                out=wraw[:],
+                in_=w2[oq * N_TILE:(oq + 1) * N_TILE, kc * KC:(kc + 1) * KC].rearrange("(t p) k -> p t k", p=P),
+            )
+            return wraw
+
+        def load_base():
+            for g in range(2):
+                nc.sync.dma_start(
+                    out=bw[:, g, :].bitcast(I32),
+                    in_=base_weight_words[g].rearrange("p n t -> p (n t)").bitcast(I32),
+                )
+
+        def quant_x():
+            xw = x_sb[:].bitcast(F32)
+            xt = tpp.tile([P, 2, 2, B], F32, tag="tp", name="xt")
+            for g in range(2):
+                for u in range(2):
+                    nc.tensor.transpose(xt[:, g, u, :], xw[:, 256 * g + u:256 * (g + 1):2], ident_f[:])
+            xg = const.tile([P, 2 * B * 4], BF16, align_bytes=64)
+            nc.vector.tensor_copy(
+                out=xg[:].bitcast(F32).rearrange("p (g b u) -> p g b u", g=2, u=2),
+                in_=xt[:].rearrange("p g u b -> p g b u"),
+            )
+            nc.vector.quantize_mx(
+                out=xcodes[:].rearrange("p g b -> p (g b)").bitcast(FP8X4),
+                scales=xscl[:].rearrange("p g b -> p (g b)"),
+                in_=xg[:],
+            )
+
+        def basis_chunk(ch):
+            xrep = bpool.tile([P, P, 4], BF16, tag="xrep", name="xrep")
+            nc.vector.tensor_copy(
+                out=xrep[:],
+                in_=x_sb[:, P * ch:P * (ch + 1)].unsqueeze(2).to_broadcast([P, P, 4]),
+            )
+            xrf = xrep[:].rearrange("p i r -> p (i r)")
+            xr = tpp.tile([P, 4, B], BF16, tag="tp", name="xr")
+            for cc in range(4):
+                nc.tensor.transpose(xr[:, cc, :], xrf[:, P * cc:P * (cc + 1)], ident_b[:])
+            s = bpool.tile([P, 2, 2, B, 2], F32, tag="s", name="s")
+            for e in range(2):
+                nc.scalar.activation(
+                    out=s[:, e], in_=xr[:].rearrange("p (g u) b -> p g b u", u=2),
+                    func=ACT.Abs, bias=cb[:, e:e + 1], scale=2.5,
+                )
+            sf = s[:].rearrange("p e g b u -> p (e g b u)")
+            nd = bpool.tile([P, 1024], F32, tag="nd", name="nd")
+            nc.vector.tensor_scalar(out=nd[:], in0=sf, scalar1=2.0, scalar2=0.0, op0=ALU.subtract, op1=ALU.min)
+            sqa = bpool.tile([P, 1024], F32, tag="sqa", name="sqa")
+            nc.scalar.activation(out=sqa[:], in_=nd[:], func=ACT.Square, scale=math.sqrt(1.0 / 6.0))
+            qh = bpool.tile([P, 1024], F32, tag="qh", name="qh")
+            nc.scalar.activation(out=qh[:], in_=sf, func=ACT.Square, scale=math.sqrt(0.5))
+            f1 = bpool.tile([P, 2, 512], F32, tag="f1", name="f1")
+            nc.vector.scalar_tensor_tensor(
+                out=f1[:].rearrange("p e n -> p (e n)"), in0=nd[:], scalar=-1.0, in1=sqa[:], op0=ALU.mult, op1=ALU.mult)
+            gg = bpool.tile([P, 2, 512], F32, tag="gg", name="gg")
+            nc.vector.tensor_tensor(out=gg[:].rearrange("p e n -> p (e n)"), in0=nd[:], in1=qh[:], op=ALU.mult)
+            bg = bpool.tile([P, 1024], BF16, tag="bg", name="bg", align_bytes=64)
+            nc.vector.scalar_tensor_tensor(
+                out=bg[:].rearrange("p (n e) -> p n e", e=2),
+                in0=gg[:].rearrange("p e n -> p n e"), scalar=2.0 / 3.0,
+                in1=f1[:].rearrange("p e n -> p n e"), op0=ALU.add, op1=ALU.min)
+            nc.vector.quantize_mx(
+                out=bcodes[:, 2 * ch:2 * ch + 2, :].rearrange("p g b -> p (g b)").bitcast(FP8X4),
+                scales=bscl[:, 2 * ch:2 * ch + 2, :].rearrange("p g b -> p (g b)"),
+                in_=bg[:],
+            )
+
+        def prep_unit(wraw):
+            ww = wraw[:].rearrange("p t k -> p (t k)").bitcast(F32)
+            res = []
+            for gl in range(PASSES_U):
+                grp = gpool.tile([P, 4 * N_TILE], BF16, tag="grp", name="grp", align_bytes=64)
+                gw = grp[:].bitcast(F32).rearrange("p (n u) -> p n u", u=2)
+                for th in range(2):
+                    bank = tpp.tile([P, 2, 2, P], F32, tag="tp", name="bank")
+                    for tt in range(2):
+                        for u in range(2):
+                            c0 = (2 * th + tt) * (KC // 2) + 256 * gl + 128 * u
+                            nc.tensor.transpose(bank[:, tt, u, :], ww[:, c0:c0 + P], ident_f[:])
+                    dst = gw[:, 256 * th:256 * (th + 1), :].rearrange("p (tt o) u -> p tt o u", tt=2)
+                    src = bank[:].rearrange("p tt u o -> p tt o u")
+                    if 2 * gl + th in VEC_BANKS:
+                        nc.vector.tensor_copy(out=dst, in_=src)
+                    else:
+                        nc.scalar.copy(out=dst, in_=src)
+                codes = cpool.tile([P, N_TILE], U32, tag="codes", name="codes", align_bytes=64)
+                scl = cpool.tile([P, N_TILE], U8, tag="scl", name="scl", align_bytes=64)
+                nc.vector.quantize_mx(out=codes[:].bitcast(FP8X4), scales=scl[:], in_=grp[:])
+                res.append((codes, scl))
+            return res
+
+        def mx_unit(kc, oq, res):
+            for gl in range(PASSES_U):
+                g = kc * PASSES_U + gl
+                codes, scl = res[gl]
+                nc.tensor.matmul_mx(
+                    out=acc[oq][:],
+                    lhsT=bcodes[:, g, :].bitcast(FP8X4), lhsT_scale=bscl[:, g, :],
+                    rhs=codes[:].bitcast(FP8X4), rhs_scale=scl[:],
+                    start=(g == 0), stop=(g == K // 512 - 1),
+                )
+
+        def mx_base(oq):
+            cols = slice(oq * N_TILE, (oq + 1) * N_TILE)
+            for g in range(2):
+                nc.tensor.matmul_mx(
+                    out=acc[oq][:],
+                    lhsT=xcodes[:, g, :].bitcast(FP8X4), lhsT_scale=xscl[:, g, :],
+                    rhs=bw[:, g, cols].bitcast(FP8X4), rhs_scale=planes[:, g, cols],
+                    start=False, stop=False,
+                )
+
+        def finish(oq):
+            res = opool.tile([P, N_TILE], F32, tag="res", name="res")
+            nc.vector.tensor_copy(out=res[:], in_=acc[oq][:])
+            nc.sync.dma_start(out=out[:, oq * N_TILE:(oq + 1) * N_TILE], in_=res[:])
+
+        units = [(kc, oq) for kc in range(N_KC) for oq in range(N_OQ)]
+        basis_chunk(0)
+        basis_chunk(1)
+        quant_x()
+        for n, (kc, oq) in enumerate(units):
+            wraw = load_unit(kc, oq)
+            if n == 3:
+                load_base()
+            res = prep_unit(wraw)
+            mx_unit(kc, oq, res)
+            if kc == 1:
+                mx_base(oq)
+            if kc < N_KC - 1 and oq in (0, 2):
+                basis_chunk(2 * (kc + 1) + oq // 2)
+            if kc == N_KC - 1:
+                finish(oq)

@@ -23,7 +23,6 @@ KC = 2048
 PASSES_U = KC // 512
 N_OQ = O // N_TILE
 N_KC = K // KC
-VEC_BANKS = (3,)
 
 
 def tile_kanlayer_w_kernel(tc, x, base_weight_words, base_weight_scales, spline_weight, out):
@@ -33,11 +32,12 @@ def tile_kanlayer_w_kernel(tc, x, base_weight_words, base_weight_scales, spline_
         const = ctx.enter_context(tc.tile_pool(name="const", bufs=1))
         wpool = ctx.enter_context(tc.tile_pool(name="wraw", bufs=4))
         gpool = ctx.enter_context(tc.tile_pool(name="grp", bufs=6))
-        cpool = ctx.enter_context(tc.tile_pool(name="codes", bufs=8))
+        cpool = ctx.enter_context(tc.tile_pool(name="codes", bufs=10))
         bpool = ctx.enter_context(tc.tile_pool(name="basis", bufs=2))
         opool = ctx.enter_context(tc.tile_pool(name="outs", bufs=2))
         accp = ctx.enter_context(tc.psum_pool(name="acc", bufs=1))
         tpp = ctx.enter_context(tc.psum_pool(name="tp", bufs=4))
+        ctx.enter_context(tc.manual_schedule())
 
         x_sb = const.tile([P, I], BF16, align_bytes=64)
         nc.sync.dma_start(out=x_sb[:], in_=x)
@@ -67,16 +67,20 @@ def tile_kanlayer_w_kernel(tc, x, base_weight_words, base_weight_scales, spline_
         xcodes = const.tile([P, 2, B], U32, align_bytes=64)
         xscl = const.tile([P, 2, B], U8, align_bytes=64)
         bw = const.tile([P, 2, O], U32, align_bytes=64)
-
+        xg = const.tile([P, 2 * B * 4], BF16, align_bytes=64)
         acc = [accp.tile([P, N_TILE], F32, name="acc%d" % q) for q in range(N_OQ)]
 
-        def load_unit(kc, oq):
+        units = [(kc, oq) for kc in range(N_KC) for oq in range(N_OQ)]
+        wtiles = {}
+
+        def load_unit(n):
+            kc, oq = units[n]
             wraw = wpool.tile([P, 4, KC], BF16, tag="wraw", name="wraw")
             nc.sync.dma_start(
                 out=wraw[:],
                 in_=w2[oq * N_TILE:(oq + 1) * N_TILE, kc * KC:(kc + 1) * KC].rearrange("(t p) k -> p t k", p=P),
             )
-            return wraw
+            wtiles[n] = wraw
 
         def load_base():
             for g in range(2):
@@ -85,125 +89,179 @@ def tile_kanlayer_w_kernel(tc, x, base_weight_words, base_weight_scales, spline_
                     in_=base_weight_words[g].rearrange("p n t -> p (n t)").bitcast(I32),
                 )
 
-        def quant_x():
-            xw = x_sb[:].bitcast(F32)
-            xt = tpp.tile([P, 2, 2, B], F32, tag="tp", name="xt")
-            for g in range(2):
-                for u in range(2):
-                    nc.tensor.transpose(xt[:, g, u, :], xw[:, 256 * g + u:256 * (g + 1):2], ident_f[:])
-            xg = const.tile([P, 2 * B * 4], BF16, align_bytes=64)
-            nc.vector.tensor_copy(
-                out=xg[:].bitcast(F32).rearrange("p (g b u) -> p g b u", g=2, u=2),
-                in_=xt[:].rearrange("p g u b -> p g b u"),
-            )
-            nc.vector.quantize_mx(
-                out=xcodes[:].rearrange("p g b -> p (g b)").bitcast(FP8X4),
-                scales=xscl[:].rearrange("p g b -> p (g b)"),
-                in_=xg[:],
-            )
+        bt = {}
 
-        def basis_chunk(ch):
+        def st_a(ch):
             xrep = bpool.tile([P, P, 4], BF16, tag="xrep", name="xrep")
-            nc.vector.tensor_copy(
-                out=xrep[:],
-                in_=x_sb[:, P * ch:P * (ch + 1)].unsqueeze(2).to_broadcast([P, P, 4]),
-            )
+            nc.vector.tensor_copy(out=xrep[:], in_=x_sb[:, P * ch:P * (ch + 1)].unsqueeze(2).to_broadcast([P, P, 4]))
             xrf = xrep[:].rearrange("p i r -> p (i r)")
             xr = tpp.tile([P, 4, B], BF16, tag="tp", name="xr")
             for cc in range(4):
                 nc.tensor.transpose(xr[:, cc, :], xrf[:, P * cc:P * (cc + 1)], ident_b[:])
             s = bpool.tile([P, 2, 2, B, 2], F32, tag="s", name="s")
             for e in range(2):
-                nc.scalar.activation(
-                    out=s[:, e], in_=xr[:].rearrange("p (g u) b -> p g b u", u=2),
-                    func=ACT.Abs, bias=cb[:, e:e + 1], scale=2.5,
-                )
-            sf = s[:].rearrange("p e g b u -> p (e g b u)")
+                nc.scalar.activation(out=s[:, e], in_=xr[:].rearrange("p (g u) b -> p g b u", u=2),
+                                     func=ACT.Abs, bias=cb[:, e:e + 1], scale=2.5)
+            bt[ch] = {"s": s}
+
+        def st_b(ch):
+            t = bt[ch]
             nd = bpool.tile([P, 1024], F32, tag="nd", name="nd")
-            nc.vector.tensor_scalar(out=nd[:], in0=sf, scalar1=2.0, scalar2=0.0, op0=ALU.subtract, op1=ALU.min)
+            nc.vector.tensor_scalar(out=nd[:], in0=t["s"][:].rearrange("p e g b u -> p (e g b u)"),
+                                    scalar1=2.0, scalar2=0.0, op0=ALU.subtract, op1=ALU.min)
             sqa = bpool.tile([P, 1024], F32, tag="sqa", name="sqa")
             nc.scalar.activation(out=sqa[:], in_=nd[:], func=ACT.Square, scale=math.sqrt(1.0 / 6.0))
+            t["nd"] = nd
+            t["sqa"] = sqa
+
+        def st_c(ch):
+            t = bt[ch]
             qh = bpool.tile([P, 1024], F32, tag="qh", name="qh")
-            nc.scalar.activation(out=qh[:], in_=sf, func=ACT.Square, scale=math.sqrt(0.5))
+            nc.scalar.activation(out=qh[:], in_=t["s"][:].rearrange("p e g b u -> p (e g b u)"),
+                                 func=ACT.Square, scale=math.sqrt(0.5))
             f1 = bpool.tile([P, 2, 512], F32, tag="f1", name="f1")
-            nc.vector.scalar_tensor_tensor(
-                out=f1[:].rearrange("p e n -> p (e n)"), in0=nd[:], scalar=-1.0, in1=sqa[:], op0=ALU.mult, op1=ALU.mult)
+            nc.vector.scalar_tensor_tensor(out=f1[:].rearrange("p e n -> p (e n)"), in0=t["nd"][:], scalar=-1.0,
+                                           in1=t["sqa"][:], op0=ALU.mult, op1=ALU.mult)
+            t["qh"] = qh
+            t["f1"] = f1
+
+        def st_d(ch):
+            t = bt[ch]
             gg = bpool.tile([P, 2, 512], F32, tag="gg", name="gg")
-            nc.vector.tensor_tensor(out=gg[:].rearrange("p e n -> p (e n)"), in0=nd[:], in1=qh[:], op=ALU.mult)
+            nc.vector.tensor_tensor(out=gg[:].rearrange("p e n -> p (e n)"), in0=t["nd"][:], in1=t["qh"][:], op=ALU.mult)
+            t["gg"] = gg
+
+        def st_e(ch):
+            t = bt[ch]
             bg = bpool.tile([P, 1024], BF16, tag="bg", name="bg", align_bytes=64)
             nc.vector.scalar_tensor_tensor(
                 out=bg[:].rearrange("p (n e) -> p n e", e=2),
-                in0=gg[:].rearrange("p e n -> p n e"), scalar=2.0 / 3.0,
-                in1=f1[:].rearrange("p e n -> p n e"), op0=ALU.add, op1=ALU.min)
+                in0=t["gg"][:].rearrange("p e n -> p n e"), scalar=2.0 / 3.0,
+                in1=t["f1"][:].rearrange("p e n -> p n e"), op0=ALU.add, op1=ALU.min)
+            t["bg"] = bg
+
+        def st_f(ch):
             nc.vector.quantize_mx(
                 out=bcodes[:, 2 * ch:2 * ch + 2, :].rearrange("p g b -> p (g b)").bitcast(FP8X4),
                 scales=bscl[:, 2 * ch:2 * ch + 2, :].rearrange("p g b -> p (g b)"),
-                in_=bg[:],
+                in_=bt[ch]["bg"][:],
             )
 
-        def prep_unit(wraw):
-            ww = wraw[:].rearrange("p t k -> p (t k)").bitcast(F32)
-            res = []
-            for gl in range(PASSES_U):
-                grp = gpool.tile([P, 4 * N_TILE], BF16, tag="grp", name="grp", align_bytes=64)
-                gw = grp[:].bitcast(F32).rearrange("p (n u) -> p n u", u=2)
-                for th in range(2):
-                    bank = tpp.tile([P, 2, 2, P], F32, tag="tp", name="bank")
-                    for tt in range(2):
-                        for u in range(2):
-                            c0 = (2 * th + tt) * (KC // 2) + 256 * gl + 128 * u
-                            nc.tensor.transpose(bank[:, tt, u, :], ww[:, c0:c0 + P], ident_f[:])
-                    dst = gw[:, 256 * th:256 * (th + 1), :].rearrange("p (tt o) u -> p tt o u", tt=2)
-                    src = bank[:].rearrange("p tt u o -> p tt o u")
-                    if 2 * gl + th in VEC_BANKS:
-                        nc.vector.tensor_copy(out=dst, in_=src)
-                    else:
-                        nc.scalar.copy(out=dst, in_=src)
+        VEC_SETS = ((), (0,), (0, 2))
+        grps = {}
+        cods = {}
+
+        def transposes_and_copies(h, n_vec):
+            n, half = h // 2, h % 2
+            ww = wtiles[n][:].rearrange("p t k -> p (t k)").bitcast(F32)
+            banks = []
+            for j in range(4):
+                gl, th = 2 * half + j // 2, j % 2
+                bank = tpp.tile([P, 2, 2, P], F32, tag="tp", name="bank")
+                for tt in range(2):
+                    for u in range(2):
+                        c0 = (2 * th + tt) * (KC // 2) + 256 * gl + 128 * u
+                        nc.tensor.transpose(bank[:, tt, u, :], ww[:, c0:c0 + P], ident_f[:])
+                banks.append(bank)
+            grps[h] = []
+            for j in range(4):
+                th = j % 2
+                if th == 0:
+                    grp = gpool.tile([P, 4 * N_TILE], BF16, tag="grp", name="grp", align_bytes=64)
+                    grps[h].append(grp)
+                gw = grps[h][-1][:].bitcast(F32).rearrange("p (n u) -> p n u", u=2)
+                dst = gw[:, 256 * th:256 * (th + 1), :].rearrange("p (tt o) u -> p tt o u", tt=2)
+                src = banks[j][:].rearrange("p tt u o -> p tt o u")
+                if j in VEC_SETS[n_vec]:
+                    nc.vector.tensor_copy(out=dst, in_=src)
+                else:
+                    nc.scalar.copy(out=dst, in_=src)
+
+        def quantise(h):
+            cods[h] = []
+            for grp in grps[h]:
                 codes = cpool.tile([P, N_TILE], U32, tag="codes", name="codes", align_bytes=64)
                 scl = cpool.tile([P, N_TILE], U8, tag="scl", name="scl", align_bytes=64)
                 nc.vector.quantize_mx(out=codes[:].bitcast(FP8X4), scales=scl[:], in_=grp[:])
-                res.append((codes, scl))
-            return res
+                cods[h].append((codes, scl))
 
-        def mx_unit(kc, oq, res):
-            for gl in range(PASSES_U):
-                g = kc * PASSES_U + gl
-                codes, scl = res[gl]
+        def passes(h):
+            n, half = h // 2, h % 2
+            kc, oq = units[n]
+            for j in range(2):
+                g = kc * PASSES_U + 2 * half + j
+                codes, scl = cods[h][j]
                 nc.tensor.matmul_mx(
                     out=acc[oq][:],
                     lhsT=bcodes[:, g, :].bitcast(FP8X4), lhsT_scale=bscl[:, g, :],
                     rhs=codes[:].bitcast(FP8X4), rhs_scale=scl[:],
                     start=(g == 0), stop=(g == K // 512 - 1),
                 )
-
-        def mx_base(oq):
-            cols = slice(oq * N_TILE, (oq + 1) * N_TILE)
-            for g in range(2):
+            if kc == 1:
+                cols = slice(oq * N_TILE, (oq + 1) * N_TILE)
                 nc.tensor.matmul_mx(
                     out=acc[oq][:],
-                    lhsT=xcodes[:, g, :].bitcast(FP8X4), lhsT_scale=xscl[:, g, :],
-                    rhs=bw[:, g, cols].bitcast(FP8X4), rhs_scale=planes[:, g, cols],
+                    lhsT=xcodes[:, half, :].bitcast(FP8X4), lhsT_scale=xscl[:, half, :],
+                    rhs=bw[:, half, cols].bitcast(FP8X4), rhs_scale=planes[:, half, cols],
                     start=False, stop=False,
                 )
+            if kc == N_KC - 1 and half == 1:
+                res = opool.tile([P, N_TILE], F32, tag="res", name="res")
+                if oq % 2 == 0:
+                    nc.scalar.copy(out=res[:], in_=acc[oq][:])
+                else:
+                    nc.vector.tensor_copy(out=res[:], in_=acc[oq][:])
+                nc.sync.dma_start(out=out[:, oq * N_TILE:(oq + 1) * N_TILE], in_=res[:])
 
-        def finish(oq):
-            res = opool.tile([P, N_TILE], F32, tag="res", name="res")
-            nc.vector.tensor_copy(out=res[:], in_=acc[oq][:])
-            nc.sync.dma_start(out=out[:, oq * N_TILE:(oq + 1) * N_TILE], in_=res[:])
+        for n in range(3):
+            load_unit(n)
+        st_a(0)
+        st_a(1)
+        xw = x_sb[:].bitcast(F32)
+        xt = tpp.tile([P, 2, 2, B], F32, tag="tp", name="xt")
+        for g in range(2):
+            for u in range(2):
+                nc.tensor.transpose(xt[:, g, u, :], xw[:, 256 * g + u:256 * (g + 1):2], ident_f[:])
+        nc.vector.tensor_copy(out=xg[:].bitcast(F32).rearrange("p (g b u) -> p g b u", g=2, u=2),
+                              in_=xt[:].rearrange("p g u b -> p g b u"))
+        st_b(0)
+        st_c(0)
+        st_b(1)
+        st_d(0)
+        st_c(1)
+        st_e(0)
+        nc.vector.quantize_mx(out=xcodes[:].rearrange("p g b -> p (g b)").bitcast(FP8X4),
+                              scales=xscl[:].rearrange("p g b -> p (g b)"), in_=xg[:])
+        st_d(1)
+        st_f(0)
+        st_e(1)
+        st_f(1)
 
-        units = [(kc, oq) for kc in range(N_KC) for oq in range(N_OQ)]
-        basis_chunk(0)
-        basis_chunk(1)
-        quant_x()
-        for n, (kc, oq) in enumerate(units):
-            wraw = load_unit(kc, oq)
-            if n == 3:
-                load_base()
-            res = prep_unit(wraw)
-            mx_unit(kc, oq, res)
-            if kc == 1:
-                mx_base(oq)
-            if kc < N_KC - 1 and oq in (0, 2):
-                basis_chunk(2 * (kc + 1) + oq // 2)
-            if kc == N_KC - 1:
-                finish(oq)
+        NH = 2 * len(units)
+        N_VEC = (1, 0, 1, 1)
+        for h in range(NH + 2):
+            if h % 2 == 0 and h // 2 + 3 < len(units):
+                load_unit(h // 2 + 3)
+                if h == 2:
+                    load_base()
+            ph = (h - 1) % 4
+            ch = (h - 1) // 4 + 2
+            busy = 1 <= h <= 26
+            if h < NH:
+                transposes_and_copies(h, N_VEC[ph] if busy else 2)
+            if 1 <= h and ph == 0 and ch <= 7:
+                st_a(ch)
+            if h >= 2:
+                passes(h - 2)
+            if 1 <= h <= NH:
+                quantise(h - 1)
+            if h >= 1:
+                if ph == 0 and 3 <= ch <= 8:
+                    st_d(ch - 1)
+                if ph == 1 and 3 <= ch <= 8:
+                    st_e(ch - 1)
+                    st_f(ch - 1)
+                if ph == 2 and ch <= 7:
+                    st_b(ch)
+                if ph == 3 and ch <= 7:
+                    st_c(ch)

@@ -31,8 +31,8 @@ def tile_kanlayer_w_kernel(tc, x, base_weight_words, base_weight_scales, spline_
     with ExitStack() as ctx:
         const = ctx.enter_context(tc.tile_pool(name="const", bufs=1))
         wpool = ctx.enter_context(tc.tile_pool(name="wraw", bufs=4))
-        gpool = ctx.enter_context(tc.tile_pool(name="grp", bufs=6))
-        cpool = ctx.enter_context(tc.tile_pool(name="codes", bufs=10))
+        gpool = ctx.enter_context(tc.tile_pool(name="grp", bufs=3))
+        cpool = ctx.enter_context(tc.tile_pool(name="codes", bufs=5))
         bpool = ctx.enter_context(tc.tile_pool(name="basis", bufs=2))
         opool = ctx.enter_context(tc.tile_pool(name="outs", bufs=2))
         accp = ctx.enter_context(tc.psum_pool(name="acc", bufs=1))
@@ -92,12 +92,9 @@ def tile_kanlayer_w_kernel(tc, x, base_weight_words, base_weight_scales, spline_
         bt = {}
 
         def st_a(ch):
-            xrep = bpool.tile([P, P, 4], BF16, tag="xrep", name="xrep")
-            nc.vector.tensor_copy(out=xrep[:], in_=x_sb[:, P * ch:P * (ch + 1)].unsqueeze(2).to_broadcast([P, P, 4]))
-            xrf = xrep[:].rearrange("p i r -> p (i r)")
-            xr = tpp.tile([P, 4, B], BF16, tag="tp", name="xr")
+            xr = tpp.tile([P, 4, B], F32, tag="tp", name="xr")
             for cc in range(4):
-                nc.tensor.transpose(xr[:, cc, :], xrf[:, P * cc:P * (cc + 1)], ident_b[:])
+                nc.tensor.matmul(xr[:, cc, :], lhsT=sel[:, cc, :], rhs=xT[:, ch, :], start=True, stop=True)
             s = bpool.tile([P, 2, 2, B, 2], F32, tag="s", name="s")
             for e in range(2):
                 nc.scalar.activation(out=s[:, e], in_=xr[:].rearrange("p (g u) b -> p g b u", u=2),
@@ -166,11 +163,11 @@ def tile_kanlayer_w_kernel(tc, x, base_weight_words, base_weight_scales, spline_
             grps[h] = []
             for j in range(4):
                 th = j % 2
-                if th == 0:
-                    grp = gpool.tile([P, 4 * N_TILE], BF16, tag="grp", name="grp", align_bytes=64)
+                if j == 0:
+                    grp = gpool.tile([P, 8 * N_TILE], BF16, tag="grp", name="grp", align_bytes=64)
                     grps[h].append(grp)
                 gw = grps[h][-1][:].bitcast(F32).rearrange("p (n u) -> p n u", u=2)
-                dst = gw[:, 256 * th:256 * (th + 1), :].rearrange("p (tt o) u -> p tt o u", tt=2)
+                dst = gw[:, 256 * j:256 * (j + 1), :].rearrange("p (tt o) u -> p tt o u", tt=2)
                 src = banks[j][:].rearrange("p tt u o -> p tt o u")
                 if j in VEC_SETS[n_vec]:
                     nc.vector.tensor_copy(out=dst, in_=src)
@@ -178,23 +175,22 @@ def tile_kanlayer_w_kernel(tc, x, base_weight_words, base_weight_scales, spline_
                     nc.scalar.copy(out=dst, in_=src)
 
         def quantise(h):
-            cods[h] = []
-            for grp in grps[h]:
-                codes = cpool.tile([P, N_TILE], U32, tag="codes", name="codes", align_bytes=64)
-                scl = cpool.tile([P, N_TILE], U8, tag="scl", name="scl", align_bytes=64)
-                nc.vector.quantize_mx(out=codes[:].bitcast(FP8X4), scales=scl[:], in_=grp[:])
-                cods[h].append((codes, scl))
+            codes = cpool.tile([P, 2 * N_TILE], U32, tag="codes", name="codes", align_bytes=64)
+            scl = cpool.tile([P, 2 * N_TILE], U8, tag="scl", name="scl", align_bytes=64)
+            nc.vector.quantize_mx(out=codes[:].bitcast(FP8X4), scales=scl[:], in_=grps[h][0][:])
+            cods[h] = (codes, scl)
 
         def passes(h):
             n, half = h // 2, h % 2
             kc, oq = units[n]
             for j in range(2):
                 g = kc * PASSES_U + 2 * half + j
-                codes, scl = cods[h][j]
+                codes, scl = cods[h]
+                cj = slice(j * N_TILE, (j + 1) * N_TILE)
                 nc.tensor.matmul_mx(
                     out=acc[oq][:],
                     lhsT=bcodes[:, g, :].bitcast(FP8X4), lhsT_scale=bscl[:, g, :],
-                    rhs=codes[:].bitcast(FP8X4), rhs_scale=scl[:],
+                    rhs=codes[:, cj].bitcast(FP8X4), rhs_scale=scl[:, cj],
                     start=(g == 0), stop=(g == K // 512 - 1),
                 )
             if kc == 1:
@@ -215,6 +211,15 @@ def tile_kanlayer_w_kernel(tc, x, base_weight_words, base_weight_scales, spline_
 
         for n in range(3):
             load_unit(n)
+        sel = const.tile([P, 4, P], BF16)
+        nc.vector.tensor_copy(out=sel[:].rearrange("p r (j q) -> p (r j) q", q=4),
+                              in_=ident_b[:].unsqueeze(2).to_broadcast([P, P, 4]))
+        xT = const.tile([P, I // P, B], BF16)
+        xtp = tpp.tile([P, I // P, B], BF16, tag="tp", name="xtp")
+        for blk in range(I // P):
+            nc.tensor.transpose(xtp[:, blk, :], x_sb[:, P * blk:P * (blk + 1)], ident_b[:])
+        nc.vector.tensor_copy(out=xT[:, 0:2, :], in_=xtp[:, 0:2, :])
+        nc.scalar.copy(out=xT[:, 2:, :], in_=xtp[:, 2:, :])
         st_a(0)
         st_a(1)
         xw = x_sb[:].bitcast(F32)
@@ -246,9 +251,9 @@ def tile_kanlayer_w_kernel(tc, x, base_weight_words, base_weight_scales, spline_
                     load_base()
             ph = (h - 1) % 4
             ch = (h - 1) // 4 + 2
-            busy = 1 <= h <= 26
+            busy = 2 <= h <= 26
             if h < NH:
-                transposes_and_copies(h, N_VEC[ph] if busy else 2)
+                transposes_and_copies(h, N_VEC[ph] if busy else (0 if h == 0 else 1))
             if 1 <= h and ph == 0 and ch <= 7:
                 st_a(ch)
             if h >= 2:

@@ -155,6 +155,8 @@ def tile_kanlayer_w_kernel(tc, x, base_weight_words, base_weight_scales, spline_
             for j in range(4):
                 gl, th = 2 * half + j // 2, j % 2
                 bank = tpp.tile([P, 2, 2, P], F32, tag="tp", name="bank")
+                if j == 2:
+                    nc.tensor.matmul(bank[:, 0, 0, :], lhsT=ident_f[:], rhs=ident_f[:], start=True, stop=True)
                 for tt in range(2):
                     for u in range(2):
                         c0 = (2 * th + tt) * (KC // 2) + 256 * gl + 128 * u

@@ -31,7 +31,7 @@ def tile_kanlayer_w_kernel(tc, x, base_weight_words, base_weight_scales, spline_
     with ExitStack() as ctx:
         const = ctx.enter_context(tc.tile_pool(name="const", bufs=1))
         wpool = ctx.enter_context(tc.tile_pool(name="wraw", bufs=4))
-        gpool = ctx.enter_context(tc.tile_pool(name="grp", bufs=3))
+        gpool = ctx.enter_context(tc.tile_pool(name="grp", bufs=4))
         cpool = ctx.enter_context(tc.tile_pool(name="codes", bufs=5))
         bpool = ctx.enter_context(tc.tile_pool(name="basis", bufs=2))
         opool = ctx.enter_context(tc.tile_pool(name="outs", bufs=2))
@@ -41,6 +41,9 @@ def tile_kanlayer_w_kernel(tc, x, base_weight_words, base_weight_scales, spline_
 
         x_sb = const.tile([P, I], BF16, align_bytes=64)
         nc.sync.dma_start(out=x_sb[:], in_=x)
+        warm = const.tile([P, 2], F32)
+        nc.vector.memset(warm[:, 0:1], 0.0)
+        nc.scalar.activation(out=warm[:, 1:2], in_=warm[:, 0:1], func=ACT.Abs)
         planes = const.tile([P, 2, O], U8, align_bytes=64)
         nc.vector.memset(planes[:].rearrange("p g n -> p (g n)").bitcast(I32), 0)
         for q in range(4):
@@ -107,15 +110,21 @@ def tile_kanlayer_w_kernel(tc, x, base_weight_words, base_weight_scales, spline_
             nc.vector.tensor_scalar(out=nd[:], in0=t["s"][:].rearrange("p e g b u -> p (e g b u)"),
                                     scalar1=2.0, scalar2=0.0, op0=ALU.subtract, op1=ALU.min)
             sqa = bpool.tile([P, 1024], F32, tag="sqa", name="sqa")
-            nc.scalar.activation(out=sqa[:], in_=nd[:], func=ACT.Square, scale=math.sqrt(1.0 / 6.0))
+            if ch < 2:
+                nc.scalar.activation(out=sqa[:], in_=nd[:], func=ACT.Square, scale=math.sqrt(1.0 / 6.0))
+            else:
+                nc.vector.scalar_tensor_tensor(out=sqa[:], in0=nd[:], scalar=1.0 / 6.0, in1=nd[:], op0=ALU.mult, op1=ALU.mult)
             t["nd"] = nd
             t["sqa"] = sqa
 
         def st_c(ch):
             t = bt[ch]
             qh = bpool.tile([P, 1024], F32, tag="qh", name="qh")
-            nc.scalar.activation(out=qh[:], in_=t["s"][:].rearrange("p e g b u -> p (e g b u)"),
-                                 func=ACT.Square, scale=math.sqrt(0.5))
+            sf = t["s"][:].rearrange("p e g b u -> p (e g b u)")
+            if ch < 6:
+                nc.scalar.activation(out=qh[:], in_=sf, func=ACT.Square, scale=math.sqrt(0.5))
+            else:
+                nc.vector.scalar_tensor_tensor(out=qh[:], in0=sf, scalar=0.5, in1=sf, op0=ALU.mult, op1=ALU.mult)
             f1 = bpool.tile([P, 2, 512], F32, tag="f1", name="f1")
             nc.vector.scalar_tensor_tensor(out=f1[:].rearrange("p e n -> p (e n)"), in0=t["nd"][:], scalar=-1.0,
                                            in1=t["sqa"][:], op0=ALU.mult, op1=ALU.mult)
@@ -155,8 +164,6 @@ def tile_kanlayer_w_kernel(tc, x, base_weight_words, base_weight_scales, spline_
             for j in range(4):
                 gl, th = 2 * half + j // 2, j % 2
                 bank = tpp.tile([P, 2, 2, P], F32, tag="tp", name="bank")
-                if j == 2:
-                    nc.tensor.matmul(bank[:, 0, 0, :], lhsT=ident_f[:], rhs=ident_f[:], start=True, stop=True)
                 for tt in range(2):
                     for u in range(2):
                         c0 = (2 * th + tt) * (KC // 2) + 256 * gl + 128 * u
@@ -179,7 +186,11 @@ def tile_kanlayer_w_kernel(tc, x, base_weight_words, base_weight_scales, spline_
         def quantise(h):
             codes = cpool.tile([P, 2 * N_TILE], U32, tag="codes", name="codes", align_bytes=64)
             scl = cpool.tile([P, 2 * N_TILE], U8, tag="scl", name="scl", align_bytes=64)
-            nc.vector.quantize_mx(out=codes[:].bitcast(FP8X4), scales=scl[:], in_=grps[h][0][:])
+            n_cuts = 2 if h == 2 * len(units) - 1 else 1
+            wq = 2 * N_TILE // n_cuts
+            for c in range(n_cuts):
+                nc.vector.quantize_mx(out=codes[:, c * wq:(c + 1) * wq].bitcast(FP8X4), scales=scl[:, c * wq:(c + 1) * wq],
+                                      in_=grps[h][0][:, 4 * c * wq:4 * (c + 1) * wq])
             cods[h] = (codes, scl)
 
         def passes(h):
@@ -220,8 +231,8 @@ def tile_kanlayer_w_kernel(tc, x, base_weight_words, base_weight_scales, spline_
         xtp = tpp.tile([P, I // P, B], BF16, tag="tp", name="xtp")
         for blk in range(I // P):
             nc.tensor.transpose(xtp[:, blk, :], x_sb[:, P * blk:P * (blk + 1)], ident_b[:])
-        nc.vector.tensor_copy(out=xT[:, 0:2, :], in_=xtp[:, 0:2, :])
-        nc.scalar.copy(out=xT[:, 2:, :], in_=xtp[:, 2:, :])
+        nc.vector.tensor_copy(out=xT[:, 0:1, :], in_=xtp[:, 0:1, :])
+        nc.scalar.copy(out=xT[:, 1:, :], in_=xtp[:, 1:, :])
         st_a(0)
         st_a(1)
         xw = x_sb[:].bitcast(F32)
@@ -245,7 +256,6 @@ def tile_kanlayer_w_kernel(tc, x, base_weight_words, base_weight_scales, spline_
         st_f(1)
 
         NH = 2 * len(units)
-        N_VEC = (1, 0, 1, 1)
         for h in range(NH + 2):
             if h % 2 == 0 and h // 2 + 3 < len(units):
                 load_unit(h // 2 + 3)
@@ -253,9 +263,8 @@ def tile_kanlayer_w_kernel(tc, x, base_weight_words, base_weight_scales, spline_
                     load_base()
             ph = (h - 1) % 4
             ch = (h - 1) // 4 + 2
-            busy = 2 <= h <= 26
             if h < NH:
-                transposes_and_copies(h, N_VEC[ph] if busy else (0 if h == 0 else 1))
+                transposes_and_copies(h, 1 if h > 26 else 0)
             if 1 <= h and ph == 0 and ch <= 7:
                 st_a(ch)
             if h >= 2:
@@ -264,11 +273,11 @@ def tile_kanlayer_w_kernel(tc, x, base_weight_words, base_weight_scales, spline_
                 quantise(h - 1)
             if h >= 1:
                 if ph == 0 and 3 <= ch <= 8:
-                    st_d(ch - 1)
-                if ph == 1 and 3 <= ch <= 8:
                     st_e(ch - 1)
                     st_f(ch - 1)
-                if ph == 2 and ch <= 7:
+                if ph == 1 and ch <= 7:
                     st_b(ch)
-                if ph == 3 and ch <= 7:
+                if ph == 2 and ch <= 7:
                     st_c(ch)
+                if ph == 3 and ch <= 7:
+                    st_d(ch)

@@ -32,7 +32,7 @@ def tile_kanlayer_w_kernel(tc, x, base_weight_words, base_weight_scales, spline_
         const = ctx.enter_context(tc.tile_pool(name="const", bufs=1))
         wpool = ctx.enter_context(tc.tile_pool(name="wraw", bufs=4))
         gpool = ctx.enter_context(tc.tile_pool(name="grp", bufs=4))
-        cpool = ctx.enter_context(tc.tile_pool(name="codes", bufs=5))
+        cpool = ctx.enter_context(tc.tile_pool(name="codes", bufs=6))
         bpool = ctx.enter_context(tc.tile_pool(name="basis", bufs=2))
         opool = ctx.enter_context(tc.tile_pool(name="outs", bufs=2))
         accp = ctx.enter_context(tc.psum_pool(name="acc", bufs=1))
@@ -121,7 +121,7 @@ def tile_kanlayer_w_kernel(tc, x, base_weight_words, base_weight_scales, spline_
             t = bt[ch]
             qh = bpool.tile([P, 1024], F32, tag="qh", name="qh")
             sf = t["s"][:].rearrange("p e g b u -> p (e g b u)")
-            if ch < 6:
+            if ch < 8:
                 nc.scalar.activation(out=qh[:], in_=sf, func=ACT.Square, scale=math.sqrt(0.5))
             else:
                 nc.vector.scalar_tensor_tensor(out=qh[:], in0=sf, scalar=0.5, in1=sf, op0=ALU.mult, op1=ALU.mult)
@@ -153,7 +153,6 @@ def tile_kanlayer_w_kernel(tc, x, base_weight_words, base_weight_scales, spline_
                 in_=bt[ch]["bg"][:],
             )
 
-        VEC_SETS = ((), (0,), (0, 2))
         grps = {}
         cods = {}
 
@@ -178,7 +177,7 @@ def tile_kanlayer_w_kernel(tc, x, base_weight_words, base_weight_scales, spline_
                 gw = grps[h][-1][:].bitcast(F32).rearrange("p (n u) -> p n u", u=2)
                 dst = gw[:, 256 * j:256 * (j + 1), :].rearrange("p (tt o) u -> p tt o u", tt=2)
                 src = banks[j][:].rearrange("p tt u o -> p tt o u")
-                if j in VEC_SETS[n_vec]:
+                if j in n_vec:
                     nc.vector.tensor_copy(out=dst, in_=src)
                 else:
                     nc.scalar.copy(out=dst, in_=src)
@@ -256,7 +255,8 @@ def tile_kanlayer_w_kernel(tc, x, base_weight_words, base_weight_scales, spline_
         st_f(1)
 
         NH = 2 * len(units)
-        for h in range(NH + 2):
+        LAG = 3
+        for h in range(NH + LAG):
             if h % 2 == 0 and h // 2 + 3 < len(units):
                 load_unit(h // 2 + 3)
                 if h == 2:
@@ -264,11 +264,11 @@ def tile_kanlayer_w_kernel(tc, x, base_weight_words, base_weight_scales, spline_
             ph = (h - 1) % 4
             ch = (h - 1) // 4 + 2
             if h < NH:
-                transposes_and_copies(h, 1 if h > 26 else 0)
+                transposes_and_copies(h, (0,) if h > 26 else ((3,) if (ph == 3 and h >= 3) else ()))
             if 1 <= h and ph == 0 and ch <= 7:
                 st_a(ch)
-            if h >= 2:
-                passes(h - 2)
+            if h >= LAG:
+                passes(h - LAG)
             if 1 <= h <= NH:
                 quantise(h - 1)
             if h >= 1:

@@ -1,5 +1,4 @@
 from contextlib import ExitStack
-import math
 
 from concourse import mybir
 from concourse.masks import make_identity
@@ -23,6 +22,7 @@ KC = 2048
 PASSES_U = KC // 512
 N_OQ = O // N_TILE
 N_KC = K // KC
+F = KC // L
 
 
 def tile_kanlayer_w_kernel(tc, x, base_weight_words, base_weight_scales, spline_weight, out):
@@ -34,6 +34,7 @@ def tile_kanlayer_w_kernel(tc, x, base_weight_words, base_weight_scales, spline_
         gpool = ctx.enter_context(tc.tile_pool(name="grp", bufs=4))
         cpool = ctx.enter_context(tc.tile_pool(name="codes", bufs=6))
         bpool = ctx.enter_context(tc.tile_pool(name="basis", bufs=2))
+        b1pool = ctx.enter_context(tc.tile_pool(name="basis1", bufs=1))
         opool = ctx.enter_context(tc.tile_pool(name="outs", bufs=2))
         accp = ctx.enter_context(tc.psum_pool(name="acc", bufs=1))
         tpp = ctx.enter_context(tc.psum_pool(name="tp", bufs=4))
@@ -41,29 +42,42 @@ def tile_kanlayer_w_kernel(tc, x, base_weight_words, base_weight_scales, spline_
 
         x_sb = const.tile([P, I], BF16, align_bytes=64)
         nc.sync.dma_start(out=x_sb[:], in_=x)
+        units = [(kc, oq) for kc in range(N_KC) for oq in range(N_OQ)]
+        wtiles = {}
+
+        def load_unit(n):
+            kc, oq = units[n]
+            wraw = wpool.tile([P, 4, KC], BF16, tag="wraw", name="wraw")
+            src = w2[oq * N_TILE:(oq + 1) * N_TILE, kc * KC:(kc + 1) * KC].rearrange("(t p) k -> p t k", p=P)
+            pieces = 2 if n in (0, len(units) - 1) else 1
+            kp = KC // pieces
+            for c in range(pieces):
+                nc.sync.dma_start(out=wraw[:, :, c * kp:(c + 1) * kp], in_=src[:, :, c * kp:(c + 1) * kp])
+            wtiles[n] = wraw
+
+        for n in range(3):
+            load_unit(n)
+
         warm = const.tile([P, 2], F32)
         nc.vector.memset(warm[:, 0:1], 0.0)
         nc.scalar.activation(out=warm[:, 1:2], in_=warm[:, 0:1], func=ACT.Abs)
-        planes = const.tile([P, 2, O], U8, align_bytes=64)
-        nc.vector.memset(planes[:].rearrange("p g n -> p (g n)").bitcast(I32), 0)
-        for q in range(4):
-            nc.sync.dma_start(
-                out=planes[32 * q:32 * q + 4, :, :].bitcast(I32),
-                in_=base_weight_scales[:, 4 * q:4 * q + 4, :].rearrange("g r n -> r g n").bitcast(I32),
-            )
+        shift = const.tile([P, 2], F32)
+        for v in range(2):
+            nc.vector.memset(shift[:, v:v + 1], -0.5 - v)
+        minus2 = const.tile([P, 1], F32)
+        nc.vector.memset(minus2[:], -2.0)
 
         ident_f = const.tile([P, P], F32)
         make_identity(nc, ident_f[:])
-        ident_b = const.tile([P, P], BF16)
-        nc.vector.tensor_copy(out=ident_b[:], in_=ident_f[:])
+        planes = const.tile([P, 2, O], U8, align_bytes=64)
+        nc.vector.memset(planes[:].rearrange("p g n -> p (g n)").bitcast(I32), 0)
+        sgn = const.tile([P, 1], F32)
         lrow = const.tile([P, 32, 4], F32)
-        for r in range(4):
-            nc.vector.memset(lrow[:, :, r], 3.5 - 2.0 * r)
+        for q in range(4):
+            nc.vector.memset(lrow[:, :, q], 4.0 * (q // 2) - 2.0)
         lsel = const.tile([P, P], F32)
         nc.vector.tensor_tensor(out=lsel[:], in0=ident_f[:], in1=lrow[:].rearrange("p a r -> p (a r)"), op=ALU.mult)
-        cb = const.tile([P, 2], F32)
-        nc.vector.tensor_reduce(out=cb[:, 0:1], in_=lsel[:], axis=AX.X, op=ALU.add)
-        nc.vector.tensor_scalar_add(out=cb[:, 1:2], in0=cb[:, 0:1], scalar1=-1.0)
+        nc.vector.tensor_reduce(out=sgn[:], in_=lsel[:], axis=AX.X, op=ALU.add)
 
         bcodes = const.tile([P, K // 512, B], U32, align_bytes=64)
         bscl = const.tile([P, K // 512, B], U8, align_bytes=64)
@@ -73,19 +87,12 @@ def tile_kanlayer_w_kernel(tc, x, base_weight_words, base_weight_scales, spline_
         xg = const.tile([P, 2 * B * 4], BF16, align_bytes=64)
         acc = [accp.tile([P, N_TILE], F32, name="acc%d" % q) for q in range(N_OQ)]
 
-        units = [(kc, oq) for kc in range(N_KC) for oq in range(N_OQ)]
-        wtiles = {}
-
-        def load_unit(n):
-            kc, oq = units[n]
-            wraw = wpool.tile([P, 4, KC], BF16, tag="wraw", name="wraw")
-            nc.sync.dma_start(
-                out=wraw[:],
-                in_=w2[oq * N_TILE:(oq + 1) * N_TILE, kc * KC:(kc + 1) * KC].rearrange("(t p) k -> p t k", p=P),
-            )
-            wtiles[n] = wraw
-
         def load_base():
+            for q in range(4):
+                nc.sync.dma_start(
+                    out=planes[32 * q:32 * q + 4, :, :].bitcast(I32),
+                    in_=base_weight_scales[:, 4 * q:4 * q + 4, :].rearrange("g r n -> r g n").bitcast(I32),
+                )
             for g in range(2):
                 nc.sync.dma_start(
                     out=bw[:, g, :].bitcast(I32),
@@ -94,64 +101,108 @@ def tile_kanlayer_w_kernel(tc, x, base_weight_words, base_weight_scales, spline_
 
         bt = {}
 
-        def st_a(ch):
-            xr = tpp.tile([P, 4, B], F32, tag="tp", name="xr")
-            for cc in range(4):
-                nc.tensor.matmul(xr[:, cc, :], lhsT=sel[:, cc, :], rhs=xT[:, ch, :], start=True, stop=True)
-            s = bpool.tile([P, 2, 2, B, 2], F32, tag="s", name="s")
-            for e in range(2):
-                nc.scalar.activation(out=s[:, e], in_=xr[:].rearrange("p (g u) b -> p g b u", u=2),
-                                     func=ACT.Abs, bias=cb[:, e:e + 1], scale=2.5)
-            bt[ch] = {"s": s}
-
-        def st_b(ch):
-            t = bt[ch]
-            nd = bpool.tile([P, 1024], F32, tag="nd", name="nd")
-            nc.vector.tensor_scalar(out=nd[:], in0=t["s"][:].rearrange("p e g b u -> p (e g b u)"),
-                                    scalar1=2.0, scalar2=0.0, op0=ALU.subtract, op1=ALU.min)
-            sqa = bpool.tile([P, 1024], F32, tag="sqa", name="sqa")
-            if ch < 2:
-                nc.scalar.activation(out=sqa[:], in_=nd[:], func=ACT.Square, scale=math.sqrt(1.0 / 6.0))
-            else:
-                nc.vector.scalar_tensor_tensor(out=sqa[:], in0=nd[:], scalar=1.0 / 6.0, in1=nd[:], op0=ALU.mult, op1=ALU.mult)
-            t["nd"] = nd
-            t["sqa"] = sqa
-
-        def st_c(ch):
-            t = bt[ch]
-            qh = bpool.tile([P, 1024], F32, tag="qh", name="qh")
-            sf = t["s"][:].rearrange("p e g b u -> p (e g b u)")
-            if ch < 8:
-                nc.scalar.activation(out=qh[:], in_=sf, func=ACT.Square, scale=math.sqrt(0.5))
-            else:
-                nc.vector.scalar_tensor_tensor(out=qh[:], in0=sf, scalar=0.5, in1=sf, op0=ALU.mult, op1=ALU.mult)
-            f1 = bpool.tile([P, 2, 512], F32, tag="f1", name="f1")
-            nc.vector.scalar_tensor_tensor(out=f1[:].rearrange("p e n -> p (e n)"), in0=t["nd"][:], scalar=-1.0,
-                                           in1=t["sqa"][:], op0=ALU.mult, op1=ALU.mult)
-            t["qh"] = qh
-            t["f1"] = f1
-
-        def st_d(ch):
-            t = bt[ch]
-            gg = bpool.tile([P, 2, 512], F32, tag="gg", name="gg")
-            nc.vector.tensor_tensor(out=gg[:].rearrange("p e n -> p (e n)"), in0=t["nd"][:], in1=t["qh"][:], op=ALU.mult)
-            t["gg"] = gg
-
-        def st_e(ch):
-            t = bt[ch]
-            bg = bpool.tile([P, 1024], BF16, tag="bg", name="bg", align_bytes=64)
+        def st_y(c):
+            y = bpool.tile([P, F, 2], F32, tag="y", name="y")
             nc.vector.scalar_tensor_tensor(
-                out=bg[:].rearrange("p (n e) -> p n e", e=2),
-                in0=t["gg"][:].rearrange("p e n -> p n e"), scalar=2.0 / 3.0,
-                in1=t["f1"][:].rearrange("p e n -> p n e"), op0=ALU.add, op1=ALU.min)
-            t["bg"] = bg
+                out=y[:], in0=x_sb[:, c * F:(c + 1) * F].unsqueeze(2).to_broadcast([P, F, 2]), scalar=2.5,
+                in1=shift[:].unsqueeze(1).to_broadcast([P, F, 2]), op0=ALU.mult, op1=ALU.add)
+            bt[c] = {"y": y}
 
-        def st_f(ch):
+        def st_r0(c):
+            z = b1pool.tile([P, 2 * F], F32, tag="z", name="z")
+            nc.scalar.activation(out=z[:], in_=bt[c]["y"][:].rearrange("p i v -> p (i v)"), func=ACT.Abs)
+            r = bpool.tile([P, 2, 2 * F], F32, tag="r", name="r")
+            nc.scalar.activation(out=r[:, 0], in_=z[:], func=ACT.Abs, bias=minus2[:])
+            bt[c]["r"] = r
+
+        def st_r2(c):
+            r = bt[c]["r"]
+            nc.vector.tensor_scalar(out=r[:, 1], in0=r[:, 0], scalar1=-1.0, scalar2=2.0, op0=ALU.mult, op1=ALU.add)
+
+        def st_m(c):
+            m = bpool.tile([P, 2, 2 * F], BF16, tag="m", name="m")
+            for h in range(2):
+                nc.vector.tensor_scalar(out=m[:, h], in0=bt[c]["y"][:].rearrange("p i v -> p (i v)"),
+                                        scalar1=2.0 * h - 2.0, scalar2=0.5, op0=ALU.is_ge, op1=ALU.subtract)
+            bt[c]["m"] = m
+
+        def st_w(c):
+            w = bpool.tile([P, 2, 2 * F], F32, tag="w", name="w")
+            nc.scalar.activation(out=w[:], in_=bt[c]["r"][:], func=ACT.Square)
+            bt[c]["w"] = w
+
+        def st_f1(c):
+            f1 = b1pool.tile([P, 2, 2 * F], F32, tag="f1", name="f1")
+            nc.vector.scalar_tensor_tensor(out=f1[:], in0=bt[c]["w"][:], scalar=1.0 / 6.0, in1=bt[c]["r"][:],
+                                           op0=ALU.mult, op1=ALU.mult)
+            bt[c]["f1"] = f1
+
+        def st_g(c):
+            g = b1pool.tile([P, 2, 2 * F], F32, tag="g", name="g")
+            for h in range(2):
+                nc.vector.scalar_tensor_tensor(out=g[:, h], in0=bt[c]["w"][:, 1 - h], scalar=-0.5,
+                                               in1=bt[c]["r"][:, h], op0=ALU.mult, op1=ALU.mult)
+            bt[c]["g"] = g
+
+        def st_b(c):
+            b = bpool.tile([P, 2, 2 * F], BF16, tag="b", name="b")
+            nc.vector.scalar_tensor_tensor(out=b[:], in0=bt[c]["g"][:], scalar=2.0 / 3.0, in1=bt[c]["f1"][:],
+                                           op0=ALU.add, op1=ALU.min)
+            bt[c]["b"] = b
+
+        def st_s(c):
+            s = b1pool.tile([P, F, 2, 2], BF16, tag="s", name="s")
+            nc.vector.tensor_tensor(out=s[:], in0=bt[c]["b"][:].rearrange("p h (i v) -> p i h v", v=2),
+                                    in1=bt[c]["m"][:].rearrange("p h (i v) -> p i h v", v=2), op=ALU.mult)
+            bt[c]["s"] = s
+
+        def st_n(c):
+            nat = b1pool.tile([P, F, 2, 4], BF16, tag="nat", name="nat", align_bytes=64)
+            nc.vector.tensor_copy(
+                out=nat[:],
+                in_=bt[c]["s"][:].rearrange("p i h v -> p i (h v)").unsqueeze(2).to_broadcast([P, F, 2, 4]))
+            bt[c]["nat"] = nat
+
+        def st_t(c):
+            words = bt[c]["nat"][:].rearrange("p i a q -> p (i a q)").bitcast(F32)
+            bt[c]["banks"] = []
+            for d in range(2):
+                bank = tpp.tile([P, 2, 2, B], F32, tag="tp", name="bbank")
+                for g in range(2):
+                    for u in range(2):
+                        c0 = 512 * d + 256 * g + 128 * u
+                        nc.tensor.transpose(bank[:, u, g, :], words[:, c0:c0 + P], ident_f[:])
+                bt[c]["banks"].append(bank)
+
+        def st_e(c):
+            bg = b1pool.tile([P, 8 * F], BF16, tag="bg", name="bg", align_bytes=64)
+            for d in range(2):
+                src = bt[c]["banks"][d][:].rearrange("p u g b -> p (u g b)").bitcast(BF16)
+                nc.vector.tensor_scalar(
+                    out=bg[:, 1024 * d:1024 * (d + 1)].rearrange("p (n u e) -> p n u e", u=2, e=2),
+                    in0=src.rearrange("p (u n e) -> p n u e", u=2, e=2),
+                    scalar1=sgn[:], scalar2=0.0, op0=ALU.mult, op1=ALU.max)
+            bt[c]["bg"] = bg
+
+        def st_q(c):
             nc.vector.quantize_mx(
-                out=bcodes[:, 2 * ch:2 * ch + 2, :].rearrange("p g b -> p (g b)").bitcast(FP8X4),
-                scales=bscl[:, 2 * ch:2 * ch + 2, :].rearrange("p g b -> p (g b)"),
-                in_=bt[ch]["bg"][:],
+                out=bcodes[:, 4 * c:4 * c + 4, :].rearrange("p g b -> p (g b)").bitcast(FP8X4),
+                scales=bscl[:, 4 * c:4 * c + 4, :].rearrange("p g b -> p (g b)"),
+                in_=bt[c]["bg"][:],
             )
+
+        def x_transposes():
+            xw = x_sb[:].bitcast(F32)
+            xt = tpp.tile([P, 2, 2, B], F32, tag="tp", name="xt")
+            for g in range(2):
+                for u in range(2):
+                    nc.tensor.transpose(xt[:, g, u, :], xw[:, 256 * g + u:256 * (g + 1):2], ident_f[:])
+            nc.scalar.copy(out=xg[:].bitcast(F32).rearrange("p (g b u) -> p g b u", g=2, u=2),
+                           in_=xt[:].rearrange("p g u b -> p g b u"))
+
+        def x_quantise():
+            nc.vector.quantize_mx(out=xcodes[:].rearrange("p g b -> p (g b)").bitcast(FP8X4),
+                                  scales=xscl[:].rearrange("p g b -> p (g b)"), in_=xg[:])
 
         grps = {}
         cods = {}
@@ -168,13 +219,10 @@ def tile_kanlayer_w_kernel(tc, x, base_weight_words, base_weight_scales, spline_
                         c0 = (2 * th + tt) * (KC // 2) + 256 * gl + 128 * u
                         nc.tensor.transpose(bank[:, tt, u, :], ww[:, c0:c0 + P], ident_f[:])
                 banks.append(bank)
-            grps[h] = []
+            grp = gpool.tile([P, 8 * N_TILE], BF16, tag="grp", name="grp", align_bytes=64)
+            grps[h] = grp
+            gw = grp[:].bitcast(F32).rearrange("p (n u) -> p n u", u=2)
             for j in range(4):
-                th = j % 2
-                if j == 0:
-                    grp = gpool.tile([P, 8 * N_TILE], BF16, tag="grp", name="grp", align_bytes=64)
-                    grps[h].append(grp)
-                gw = grps[h][-1][:].bitcast(F32).rearrange("p (n u) -> p n u", u=2)
                 dst = gw[:, 256 * j:256 * (j + 1), :].rearrange("p (tt o) u -> p tt o u", tt=2)
                 src = banks[j][:].rearrange("p tt u o -> p tt o u")
                 if j in n_vec:
@@ -189,7 +237,7 @@ def tile_kanlayer_w_kernel(tc, x, base_weight_words, base_weight_scales, spline_
             wq = 2 * N_TILE // n_cuts
             for c in range(n_cuts):
                 nc.vector.quantize_mx(out=codes[:, c * wq:(c + 1) * wq].bitcast(FP8X4), scales=scl[:, c * wq:(c + 1) * wq],
-                                      in_=grps[h][0][:, 4 * c * wq:4 * (c + 1) * wq])
+                                      in_=grps[h][:, 4 * c * wq:4 * (c + 1) * wq])
             cods[h] = (codes, scl)
 
         def passes(h):
@@ -221,38 +269,18 @@ def tile_kanlayer_w_kernel(tc, x, base_weight_words, base_weight_scales, spline_
                     nc.vector.tensor_copy(out=res[:], in_=acc[oq][:])
                 nc.sync.dma_start(out=out[:, oq * N_TILE:(oq + 1) * N_TILE], in_=res[:])
 
-        for n in range(3):
-            load_unit(n)
-        sel = const.tile([P, 4, P], BF16)
-        nc.vector.tensor_copy(out=sel[:].rearrange("p r (j q) -> p (r j) q", q=4),
-                              in_=ident_b[:].unsqueeze(2).to_broadcast([P, P, 4]))
-        xT = const.tile([P, I // P, B], BF16)
-        xtp = tpp.tile([P, I // P, B], BF16, tag="tp", name="xtp")
-        for blk in range(I // P):
-            nc.tensor.transpose(xtp[:, blk, :], x_sb[:, P * blk:P * (blk + 1)], ident_b[:])
-        nc.vector.tensor_copy(out=xT[:, 0:1, :], in_=xtp[:, 0:1, :])
-        nc.scalar.copy(out=xT[:, 1:, :], in_=xtp[:, 1:, :])
-        st_a(0)
-        st_a(1)
-        xw = x_sb[:].bitcast(F32)
-        xt = tpp.tile([P, 2, 2, B], F32, tag="tp", name="xt")
-        for g in range(2):
-            for u in range(2):
-                nc.tensor.transpose(xt[:, g, u, :], xw[:, 256 * g + u:256 * (g + 1):2], ident_f[:])
-        nc.vector.tensor_copy(out=xg[:].bitcast(F32).rearrange("p (g b u) -> p g b u", g=2, u=2),
-                              in_=xt[:].rearrange("p g u b -> p g b u"))
+        st_y(0)
+        st_r0(0)
+        st_y(1)
+        st_m(0)
+        st_r2(0)
+        st_w(0)
+        st_m(1)
+        st_f1(0)
+        st_g(0)
         st_b(0)
-        st_c(0)
-        st_b(1)
-        st_d(0)
-        st_c(1)
-        st_e(0)
-        nc.vector.quantize_mx(out=xcodes[:].rearrange("p g b -> p (g b)").bitcast(FP8X4),
-                              scales=xscl[:].rearrange("p g b -> p (g b)"), in_=xg[:])
-        st_d(1)
-        st_f(0)
-        st_e(1)
-        st_f(1)
+        st_s(0)
+        st_n(0)
 
         NH = 2 * len(units)
         LAG = 3
@@ -261,23 +289,45 @@ def tile_kanlayer_w_kernel(tc, x, base_weight_words, base_weight_scales, spline_
                 load_unit(h // 2 + 3)
                 if h == 2:
                     load_base()
-            ph = (h - 1) % 4
-            ch = (h - 1) // 4 + 2
+            ph = h % 8
+            c = h // 8 + 1
             if h < NH:
-                transposes_and_copies(h, (0,) if h > 26 else ((3,) if (ph == 3 and h >= 3) else ()))
-            if 1 <= h and ph == 0 and ch <= 7:
-                st_a(ch)
+                transposes_and_copies(h, (0,) if (h > 26 or ph == 3) else ())
+            if h == 2:
+                st_t(0)
+                st_e(0)
+                st_q(0)
+            if h == 4:
+                x_transposes()
+            if ph == 1 and c < N_KC:
+                st_r0(c)
+            if ph == 3 and c < N_KC:
+                st_w(c)
             if h >= LAG:
                 passes(h - LAG)
+            if ph == 0 and 1 < c <= N_KC:
+                st_t(c - 1)
+            if ph == 1 and 1 < c <= N_KC:
+                st_e(c - 1)
             if 1 <= h <= NH:
                 quantise(h - 1)
-            if h >= 1:
-                if ph == 0 and 3 <= ch <= 8:
-                    st_e(ch - 1)
-                    st_f(ch - 1)
-                if ph == 1 and ch <= 7:
-                    st_b(ch)
-                if ph == 2 and ch <= 7:
-                    st_c(ch)
-                if ph == 3 and ch <= 7:
-                    st_d(ch)
+            if h == 5:
+                x_quantise()
+            if ph == 2 and 1 < c <= N_KC:
+                st_q(c - 1)
+            if c < N_KC:
+                if ph == 0 and c > 1:
+                    st_y(c)
+                if ph == 2:
+                    st_r2(c)
+                    if c > 1:
+                        st_m(c)
+                if ph == 4:
+                    st_f1(c)
+                if ph == 5:
+                    st_g(c)
+                if ph == 6:
+                    st_b(c)
+                if ph == 7:
+                    st_s(c)
+                    st_n(c)

@@ -23,6 +23,14 @@ PASSES_U = KC // 512
 N_OQ = O // N_TILE
 N_KC = K // KC
 F = KC // L
+BANK_ORDER = (0, 2, 1, 3)
+K_PARTS = ((0, 1, 2, 3),)
+OQ_SETS = ((0, 1, 2), (3,))
+N_ACC = 3
+BASE_KC = 2
+LAG = 4
+LAG0 = 5
+GROUP = 2
 
 
 def tile_kanlayer_w_kernel(tc, x, base_weight_words, base_weight_scales, spline_weight, out):
@@ -32,27 +40,31 @@ def tile_kanlayer_w_kernel(tc, x, base_weight_words, base_weight_scales, spline_
         const = ctx.enter_context(tc.tile_pool(name="const", bufs=1))
         wpool = ctx.enter_context(tc.tile_pool(name="wraw", bufs=4))
         gpool = ctx.enter_context(tc.tile_pool(name="grp", bufs=4))
-        cpool = ctx.enter_context(tc.tile_pool(name="codes", bufs=6))
+        cpool = ctx.enter_context(tc.tile_pool(name="codes", bufs=8))
         bpool = ctx.enter_context(tc.tile_pool(name="basis", bufs=2))
         b1pool = ctx.enter_context(tc.tile_pool(name="basis1", bufs=1))
-        opool = ctx.enter_context(tc.tile_pool(name="outs", bufs=2))
-        accp = ctx.enter_context(tc.psum_pool(name="acc", bufs=1))
-        tpp = ctx.enter_context(tc.psum_pool(name="tp", bufs=4))
+        accp = ctx.enter_context(tc.psum_pool(name="acc", bufs=N_ACC))
+        tpp = ctx.enter_context(tc.psum_pool(name="tp", bufs=8 - N_ACC))
         ctx.enter_context(tc.manual_schedule())
 
         x_sb = const.tile([P, I], BF16, align_bytes=64)
         nc.sync.dma_start(out=x_sb[:], in_=x)
-        units = [(kc, oq) for kc in range(N_KC) for oq in range(N_OQ)]
+        units = [(kc, oq) for kcs in K_PARTS for oqs in OQ_SETS for kc in kcs for oq in oqs]
+        first_kc = [kcs[0] for kcs in K_PARTS]
+        last_kc = [kcs[-1] for kcs in K_PARTS]
         wtiles = {}
 
         def load_unit(n):
             kc, oq = units[n]
             wraw = wpool.tile([P, 4, KC], BF16, tag="wraw", name="wraw")
             src = w2[oq * N_TILE:(oq + 1) * N_TILE, kc * KC:(kc + 1) * KC].rearrange("(t p) k -> p t k", p=P)
-            pieces = 2 if n in (0, len(units) - 1) else 1
-            kp = KC // pieces
-            for c in range(pieces):
-                nc.sync.dma_start(out=wraw[:, :, c * kp:(c + 1) * kp], in_=src[:, :, c * kp:(c + 1) * kp])
+            k_pieces = 2 if n in (0, len(units) - 1) else 1
+            t_pieces = 2 if n == 0 else 1
+            kp, tp = KC // k_pieces, 4 // t_pieces
+            for c in range(k_pieces):
+                for d in range(t_pieces):
+                    part = (slice(None), slice(d * tp, (d + 1) * tp), slice(c * kp, (c + 1) * kp))
+                    nc.sync.dma_start(out=wraw[part], in_=src[part])
             wtiles[n] = wraw
 
         for n in range(3):
@@ -85,7 +97,9 @@ def tile_kanlayer_w_kernel(tc, x, base_weight_words, base_weight_scales, spline_
         xscl = const.tile([P, 2, B], U8, align_bytes=64)
         bw = const.tile([P, 2, O], U32, align_bytes=64)
         xg = const.tile([P, 2 * B * 4], BF16, align_bytes=64)
-        acc = [accp.tile([P, N_TILE], F32, name="acc%d" % q) for q in range(N_OQ)]
+        sums = const.tile([P, O], F32, align_bytes=64)
+        acc = {}
+        closed = []
 
         def load_base():
             for q in range(4):
@@ -207,22 +221,24 @@ def tile_kanlayer_w_kernel(tc, x, base_weight_words, base_weight_scales, spline_
         grps = {}
         cods = {}
 
-        def transposes_and_copies(h, n_vec):
+        def transposes_and_copies(h, n_vec, between=None):
             n, half = h // 2, h % 2
             ww = wtiles[n][:].rearrange("p t k -> p (t k)").bitcast(F32)
-            banks = []
-            for j in range(4):
+            banks = {}
+            for j in BANK_ORDER:
                 gl, th = 2 * half + j // 2, j % 2
                 bank = tpp.tile([P, 2, 2, P], F32, tag="tp", name="bank")
                 for tt in range(2):
                     for u in range(2):
                         c0 = (2 * th + tt) * (KC // 2) + 256 * gl + 128 * u
                         nc.tensor.transpose(bank[:, tt, u, :], ww[:, c0:c0 + P], ident_f[:])
-                banks.append(bank)
+                banks[j] = bank
             grp = gpool.tile([P, 8 * N_TILE], BF16, tag="grp", name="grp", align_bytes=64)
             grps[h] = grp
             gw = grp[:].bitcast(F32).rearrange("p (n u) -> p n u", u=2)
-            for j in range(4):
+            for i, j in enumerate(BANK_ORDER):
+                if i == 1 and between:
+                    between()
                 dst = gw[:, 256 * j:256 * (j + 1), :].rearrange("p (tt o) u -> p tt o u", tt=2)
                 src = banks[j][:].rearrange("p tt u o -> p tt o u")
                 if j in n_vec:
@@ -243,91 +259,103 @@ def tile_kanlayer_w_kernel(tc, x, base_weight_words, base_weight_scales, spline_
         def passes(h):
             n, half = h // 2, h % 2
             kc, oq = units[n]
+            opens = kc in first_kc and half == 0
+            closes = kc in last_kc and half == 1
+            cols = slice(oq * N_TILE, (oq + 1) * N_TILE)
+            if opens:
+                acc_tile = accp.tile([P, N_TILE], F32, tag="acc", name="acc")
+                acc[oq] = acc_tile
+            codes, scl = cods[h]
             for j in range(2):
                 g = kc * PASSES_U + 2 * half + j
-                codes, scl = cods[h]
                 cj = slice(j * N_TILE, (j + 1) * N_TILE)
                 nc.tensor.matmul_mx(
                     out=acc[oq][:],
                     lhsT=bcodes[:, g, :].bitcast(FP8X4), lhsT_scale=bscl[:, g, :],
                     rhs=codes[:, cj].bitcast(FP8X4), rhs_scale=scl[:, cj],
-                    start=(g == 0), stop=(g == K // 512 - 1),
+                    start=(opens and j == 0), stop=(closes and j == 1),
                 )
-            if kc == 1:
+                if j == 0 and kc == BASE_KC:
+                    nc.tensor.matmul_mx(
+                        out=acc[oq][:],
+                        lhsT=xcodes[:, half, :].bitcast(FP8X4), lhsT_scale=xscl[:, half, :],
+                        rhs=bw[:, half, cols].bitcast(FP8X4), rhs_scale=planes[:, half, cols],
+                        start=False, stop=False,
+                    )
+            if closes:
+                closed.append((oq, kc))
+
+        def empty_sums():
+            while closed:
+                oq, kc = closed.pop(0)
                 cols = slice(oq * N_TILE, (oq + 1) * N_TILE)
-                nc.tensor.matmul_mx(
-                    out=acc[oq][:],
-                    lhsT=xcodes[:, half, :].bitcast(FP8X4), lhsT_scale=xscl[:, half, :],
-                    rhs=bw[:, half, cols].bitcast(FP8X4), rhs_scale=planes[:, half, cols],
-                    start=False, stop=False,
-                )
-            if kc == N_KC - 1 and half == 1:
-                res = opool.tile([P, N_TILE], F32, tag="res", name="res")
-                if oq % 2 == 0:
-                    nc.scalar.copy(out=res[:], in_=acc[oq][:])
+                if kc == N_KC - 1:
+                    if len(K_PARTS) > 1:
+                        nc.vector.tensor_tensor(out=sums[:, cols], in0=acc[oq][:], in1=sums[:, cols], op=ALU.add)
+                    else:
+                        nc.vector.tensor_copy(out=sums[:, cols], in_=acc[oq][:])
+                    nc.sync.dma_start(out=out[:, cols], in_=sums[:, cols])
                 else:
-                    nc.vector.tensor_copy(out=res[:], in_=acc[oq][:])
-                nc.sync.dma_start(out=out[:, oq * N_TILE:(oq + 1) * N_TILE], in_=res[:])
+                    nc.scalar.copy(out=sums[:, cols], in_=acc[oq][:])
 
         st_y(0)
         st_r0(0)
         st_y(1)
         st_m(0)
         st_r2(0)
-        st_w(0)
-        st_m(1)
-        st_f1(0)
-        st_g(0)
-        st_b(0)
-        st_s(0)
-        st_n(0)
 
         NH = 2 * len(units)
-        LAG = 3
+        next_pass = [0]
+
+        def passes_up_to(last):
+            while next_pass[0] <= last:
+                passes(next_pass[0])
+                next_pass[0] += 1
+
+        plan = {}
+        for c, steps in ((1, (None, 1, 1, None, 2, 3, 4, 5, 6, 6, 7, 8, 8)), (2, (4, 5, 6, 6, 7, 8, 9, 10, 11, 11, 12, 13, 14)), (3, (10, 11, 12, 12, 13, 14, 15, 16, 17, 17, 18, 19, 20))):
+            for (at, fn), h in zip((("v", st_y), ("s", st_r0), ("v", st_r2), ("v", st_m), ("s", st_w), ("v", st_f1), ("v", st_g), ("v", st_b), ("v", st_s), ("v", st_n), ("t", st_t), ("e", st_e), ("v", st_q)), steps):
+                if h is not None:
+                    plan.setdefault((h, at), []).append((fn, c))
+
+        def run(h, at):
+            for fn, c in plan.get((h, at), ()):
+                fn(c)
+
         for h in range(NH + LAG):
             if h % 2 == 0 and h // 2 + 3 < len(units):
                 load_unit(h // 2 + 3)
-                if h == 2:
+                if h == 8:
                     load_base()
-            ph = h % 8
-            c = h // 8 + 1
-            if h < NH:
-                transposes_and_copies(h, (0,) if (h > 26 or ph == 3) else ())
-            if h == 2:
+            run(h, "e")
+            flush = list(closed)
+            if h == 0:
+                transposes_and_copies(0, (), lambda: st_w(0))
+                st_m(1)
+                st_f1(0)
+                st_g(0)
+            elif h < NH:
+                transposes_and_copies(h, (0,) if h > 20 else ())
+            if h == 3:
                 st_t(0)
-                st_e(0)
-                st_q(0)
-            if h == 4:
+            if h == 7:
                 x_transposes()
-            if ph == 1 and c < N_KC:
-                st_r0(c)
-            if ph == 3 and c < N_KC:
-                st_w(c)
-            if h >= LAG:
-                passes(h - LAG)
-            if ph == 0 and 1 < c <= N_KC:
-                st_t(c - 1)
-            if ph == 1 and 1 < c <= N_KC:
-                st_e(c - 1)
+            run(h, "s")
+            if h >= LAG0 and (h % GROUP == 0 or h >= NH):
+                passes_up_to(min(h - LAG, 2 * (h - LAG0) + 1) if h < NH else h - LAG)
+            run(h, "t")
             if 1 <= h <= NH:
                 quantise(h - 1)
-            if h == 5:
+            if h == 1:
+                st_b(0)
+            if h == 2:
+                st_s(0)
+                st_n(0)
+            if h == 3:
+                st_e(0)
+                st_q(0)
+            if h == 7 + 1:
                 x_quantise()
-            if ph == 2 and 1 < c <= N_KC:
-                st_q(c - 1)
-            if c < N_KC:
-                if ph == 0 and c > 1:
-                    st_y(c)
-                if ph == 2:
-                    st_r2(c)
-                    if c > 1:
-                        st_m(c)
-                if ph == 4:
-                    st_f1(c)
-                if ph == 5:
-                    st_g(c)
-                if ph == 6:
-                    st_b(c)
-                if ph == 7:
-                    st_s(c)
-                    st_n(c)
+            if flush or h >= NH:
+                empty_sums()
+            run(h, "v")

@@ -30,7 +30,7 @@ N_ACC = 3
 BASE_KC = 2
 LAG = 4
 LAG0 = 5
-GROUP = 2
+GROUP = 1
 
 
 def tile_kanlayer_w_kernel(tc, x, base_weight_words, base_weight_scales, spline_weight, out):
@@ -40,7 +40,7 @@ def tile_kanlayer_w_kernel(tc, x, base_weight_words, base_weight_scales, spline_
         const = ctx.enter_context(tc.tile_pool(name="const", bufs=1))
         wpool = ctx.enter_context(tc.tile_pool(name="wraw", bufs=4))
         gpool = ctx.enter_context(tc.tile_pool(name="grp", bufs=4))
-        cpool = ctx.enter_context(tc.tile_pool(name="codes", bufs=8))
+        cpool = ctx.enter_context(tc.tile_pool(name="codes", bufs=7))
         bpool = ctx.enter_context(tc.tile_pool(name="basis", bufs=2))
         b1pool = ctx.enter_context(tc.tile_pool(name="basis1", bufs=1))
         accp = ctx.enter_context(tc.psum_pool(name="acc", bufs=N_ACC))

@@ -24,9 +24,8 @@ N_OQ = O // N_TILE
 N_KC = K // KC
 F = KC // L
 BANK_ORDER = (0, 2, 1, 3)
-K_PARTS = ((0, 1, 2, 3),)
-OQ_SETS = ((0, 1, 2), (3,))
-N_ACC = 3
+PARTS = (((0, 1, 2, 3), (0, 1, 2)), ((0, 1, 2, 3), (3,)))
+CLOSES = ((3,), (3,), (3,), (3,))
 BASE_KC = 2
 LAG = 4
 LAG0 = 5
@@ -40,25 +39,29 @@ def tile_kanlayer_w_kernel(tc, x, base_weight_words, base_weight_scales, spline_
         const = ctx.enter_context(tc.tile_pool(name="const", bufs=1))
         wpool = ctx.enter_context(tc.tile_pool(name="wraw", bufs=4))
         gpool = ctx.enter_context(tc.tile_pool(name="grp", bufs=4))
-        cpool = ctx.enter_context(tc.tile_pool(name="codes", bufs=7))
+        cpool = ctx.enter_context(tc.tile_pool(name="codes", bufs=8))
         bpool = ctx.enter_context(tc.tile_pool(name="basis", bufs=2))
         b1pool = ctx.enter_context(tc.tile_pool(name="basis1", bufs=1))
-        accp = ctx.enter_context(tc.psum_pool(name="acc", bufs=N_ACC))
-        tpp = ctx.enter_context(tc.psum_pool(name="tp", bufs=8 - N_ACC))
+        psum = ctx.enter_context(tc.psum_pool(name="psum", bufs=1))
         ctx.enter_context(tc.manual_schedule())
 
         x_sb = const.tile([P, I], BF16, align_bytes=64)
         nc.sync.dma_start(out=x_sb[:], in_=x)
-        units = [(kc, oq) for kcs in K_PARTS for oqs in OQ_SETS for kc in kcs for oq in oqs]
-        first_kc = [kcs[0] for kcs in K_PARTS]
-        last_kc = [kcs[-1] for kcs in K_PARTS]
+        units = [(kc, oq) for kcs, oqs in PARTS for kc in kcs for oq in oqs]
+        free_banks = ["bank%d" % i for i in range(8)]
+
+        def transposes_bank():
+            tag = free_banks.pop(0)
+            free_banks.append(tag)
+            bank = psum.tile([P, 2, 2, P], F32, tag=tag, name="bank")
+            return bank
         wtiles = {}
 
         def load_unit(n):
             kc, oq = units[n]
             wraw = wpool.tile([P, 4, KC], BF16, tag="wraw", name="wraw")
             src = w2[oq * N_TILE:(oq + 1) * N_TILE, kc * KC:(kc + 1) * KC].rearrange("(t p) k -> p t k", p=P)
-            k_pieces = 2 if n in (0, len(units) - 1) else 1
+            k_pieces = 2 if n < 2 or n == len(units) - 1 else 1
             t_pieces = 2 if n == 0 else 1
             kp, tp = KC // k_pieces, 4 // t_pieces
             for c in range(k_pieces):
@@ -99,6 +102,7 @@ def tile_kanlayer_w_kernel(tc, x, base_weight_words, base_weight_scales, spline_
         xg = const.tile([P, 2 * B * 4], BF16, align_bytes=64)
         sums = const.tile([P, O], F32, align_bytes=64)
         acc = {}
+        acc_tag = {}
         closed = []
 
         def load_base():
@@ -142,7 +146,9 @@ def tile_kanlayer_w_kernel(tc, x, base_weight_words, base_weight_scales, spline_
 
         def st_w(c):
             w = bpool.tile([P, 2, 2 * F], F32, tag="w", name="w")
-            nc.scalar.activation(out=w[:], in_=bt[c]["r"][:], func=ACT.Square)
+            r0 = bt[c]["r"][:, 0]
+            nc.scalar.activation(out=w[:, 0], in_=r0, func=ACT.Square)
+            nc.scalar.activation(out=w[:, 1], in_=r0, func=ACT.Square, bias=minus2[:])
             bt[c]["w"] = w
 
         def st_f1(c):
@@ -181,7 +187,7 @@ def tile_kanlayer_w_kernel(tc, x, base_weight_words, base_weight_scales, spline_
             words = bt[c]["nat"][:].rearrange("p i a q -> p (i a q)").bitcast(F32)
             bt[c]["banks"] = []
             for d in range(2):
-                bank = tpp.tile([P, 2, 2, B], F32, tag="tp", name="bbank")
+                bank = transposes_bank()
                 for g in range(2):
                     for u in range(2):
                         c0 = 512 * d + 256 * g + 128 * u
@@ -207,7 +213,7 @@ def tile_kanlayer_w_kernel(tc, x, base_weight_words, base_weight_scales, spline_
 
         def x_transposes():
             xw = x_sb[:].bitcast(F32)
-            xt = tpp.tile([P, 2, 2, B], F32, tag="tp", name="xt")
+            xt = transposes_bank()
             for g in range(2):
                 for u in range(2):
                     nc.tensor.transpose(xt[:, g, u, :], xw[:, 256 * g + u:256 * (g + 1):2], ident_f[:])
@@ -227,7 +233,7 @@ def tile_kanlayer_w_kernel(tc, x, base_weight_words, base_weight_scales, spline_
             banks = {}
             for j in BANK_ORDER:
                 gl, th = 2 * half + j // 2, j % 2
-                bank = tpp.tile([P, 2, 2, P], F32, tag="tp", name="bank")
+                bank = transposes_bank()
                 for tt in range(2):
                     for u in range(2):
                         c0 = (2 * th + tt) * (KC // 2) + 256 * gl + 128 * u
@@ -259,11 +265,12 @@ def tile_kanlayer_w_kernel(tc, x, base_weight_words, base_weight_scales, spline_
         def passes(h):
             n, half = h // 2, h % 2
             kc, oq = units[n]
-            opens = kc in first_kc and half == 0
-            closes = kc in last_kc and half == 1
+            opens = half == 0 and (kc == 0 or kc - 1 in CLOSES[oq])
+            closes = half == 1 and kc in CLOSES[oq]
             cols = slice(oq * N_TILE, (oq + 1) * N_TILE)
             if opens:
-                acc_tile = accp.tile([P, N_TILE], F32, tag="acc", name="acc")
+                acc_tag[oq] = free_banks.pop(0)
+                acc_tile = psum.tile([P, N_TILE], F32, tag=acc_tag[oq], name="acc")
                 acc[oq] = acc_tile
             codes, scl = cods[h]
             for j in range(2):
@@ -289,14 +296,15 @@ def tile_kanlayer_w_kernel(tc, x, base_weight_words, base_weight_scales, spline_
             while closed:
                 oq, kc = closed.pop(0)
                 cols = slice(oq * N_TILE, (oq + 1) * N_TILE)
-                if kc == N_KC - 1:
-                    if len(K_PARTS) > 1:
-                        nc.vector.tensor_tensor(out=sums[:, cols], in0=acc[oq][:], in1=sums[:, cols], op=ALU.add)
-                    else:
-                        nc.vector.tensor_copy(out=sums[:, cols], in_=acc[oq][:])
-                    nc.sync.dma_start(out=out[:, cols], in_=sums[:, cols])
+                if kc != CLOSES[oq][0]:
+                    nc.vector.tensor_tensor(out=sums[:, cols], in0=acc[oq][:], in1=sums[:, cols], op=ALU.add)
+                elif kc == N_KC - 1:
+                    nc.vector.tensor_copy(out=sums[:, cols], in_=acc[oq][:])
                 else:
                     nc.scalar.copy(out=sums[:, cols], in_=acc[oq][:])
+                if kc == N_KC - 1:
+                    nc.sync.dma_start(out=out[:, cols], in_=sums[:, cols])
+                free_banks.append(acc_tag[oq])
 
         st_y(0)
         st_r0(0)
@@ -313,7 +321,7 @@ def tile_kanlayer_w_kernel(tc, x, base_weight_words, base_weight_scales, spline_
                 next_pass[0] += 1
 
         plan = {}
-        for c, steps in ((1, (None, 1, 1, None, 2, 3, 4, 5, 6, 6, 7, 8, 8)), (2, (4, 5, 6, 6, 7, 8, 9, 10, 11, 11, 12, 13, 14)), (3, (10, 11, 12, 12, 13, 14, 15, 16, 17, 17, 18, 19, 20))):
+        for c, steps in ((1, (None, 1, None, None, 2, None, 4, 5, 6, 7, 8, 9, 9)), (2, (5, 6, 7, 7, 8, 9, 10, 11, 12, 13, 14, 15, 15)), (3, (11, 12, 13, 13, 14, 15, 16, 17, 18, 19, 20, 21, 21))):
             for (at, fn), h in zip((("v", st_y), ("s", st_r0), ("v", st_r2), ("v", st_m), ("s", st_w), ("v", st_f1), ("v", st_g), ("v", st_b), ("v", st_s), ("v", st_n), ("t", st_t), ("e", st_e), ("v", st_q)), steps):
                 if h is not None:
                     plan.setdefault((h, at), []).append((fn, c))
@@ -331,28 +339,30 @@ def tile_kanlayer_w_kernel(tc, x, base_weight_words, base_weight_scales, spline_
             flush = list(closed)
             if h == 0:
                 transposes_and_copies(0, (), lambda: st_w(0))
-                st_m(1)
                 st_f1(0)
                 st_g(0)
             elif h < NH:
-                transposes_and_copies(h, (0,) if h > 20 else ())
+                transposes_and_copies(h, (0,) if h > 24 else ())
             if h == 3:
                 st_t(0)
             if h == 7:
                 x_transposes()
             run(h, "s")
-            if h >= LAG0 and (h % GROUP == 0 or h >= NH):
+            if h >= LAG0 and (h < 24 or h % 2 == 0 or h >= NH):
                 passes_up_to(min(h - LAG, 2 * (h - LAG0) + 1) if h < NH else h - LAG)
             run(h, "t")
             if 1 <= h <= NH:
                 quantise(h - 1)
             if h == 1:
                 st_b(0)
+                st_m(1)
             if h == 2:
                 st_s(0)
+                st_r2(1)
                 st_n(0)
             if h == 3:
                 st_e(0)
+                st_f1(1)
                 st_q(0)
             if h == 7 + 1:
                 x_quantise()

@@ -24,8 +24,6 @@ N_OQ = O // N_TILE
 N_KC = K // KC
 F = KC // L
 BANK_ORDER = (0, 2, 1, 3)
-PARTS = (((0, 1, 2, 3), (0, 1, 2)), ((0, 1, 2, 3), (3,)))
-CLOSES = ((3,), (3,), (3,), (3,))
 BASE_KC = 2
 LAG = 4
 LAG0 = 5
@@ -47,7 +45,9 @@ def tile_kanlayer_w_kernel(tc, x, base_weight_words, base_weight_scales, spline_
 
         x_sb = const.tile([P, I], BF16, align_bytes=64)
         nc.sync.dma_start(out=x_sb[:], in_=x)
-        units = [(kc, oq) for kcs, oqs in PARTS for kc in kcs for oq in oqs]
+        units = [(kc, oq) for kc in range(N_KC) for oq in range(N_OQ - 1)]
+        n_tiles = len(units)
+        units += [(None, t) for t in range(4)]
         free_banks = ["bank%d" % i for i in range(8)]
 
         def transposes_bank():
@@ -60,8 +60,17 @@ def tile_kanlayer_w_kernel(tc, x, base_weight_words, base_weight_scales, spline_
         def load_unit(n):
             kc, oq = units[n]
             wraw = wpool.tile([P, 4, KC], BF16, tag="wraw", name="wraw")
+            wtiles[n] = wraw
+            if kc is None:
+                o0 = (N_OQ - 1) * N_TILE + P * oq
+                k_pieces = 2 if n == len(units) - 1 else 1
+                row = wraw[:].rearrange("p t k -> p (t k)")
+                for c in range(k_pieces):
+                    ks = slice(c * K // k_pieces, (c + 1) * K // k_pieces)
+                    nc.sync.dma_start(out=row[:, ks], in_=w2[o0:o0 + P, ks])
+                return
             src = w2[oq * N_TILE:(oq + 1) * N_TILE, kc * KC:(kc + 1) * KC].rearrange("(t p) k -> p t k", p=P)
-            k_pieces = 2 if n < 2 or n == len(units) - 1 else 1
+            k_pieces = 2 if n < 2 else 1
             t_pieces = 2 if n == 0 else 1
             kp, tp = KC // k_pieces, 4 // t_pieces
             for c in range(k_pieces):
@@ -231,18 +240,21 @@ def tile_kanlayer_w_kernel(tc, x, base_weight_words, base_weight_scales, spline_
             n, half = h // 2, h % 2
             ww = wtiles[n][:].rearrange("p t k -> p (t k)").bitcast(F32)
             banks = {}
-            for j in BANK_ORDER:
+            for j in (BANK_ORDER if h < 2 else range(4)):
                 gl, th = 2 * half + j // 2, j % 2
                 bank = transposes_bank()
                 for tt in range(2):
                     for u in range(2):
-                        c0 = (2 * th + tt) * (KC // 2) + 256 * gl + 128 * u
+                        if n < n_tiles:
+                            c0 = (2 * th + tt) * (KC // 2) + 256 * gl + 128 * u
+                        else:
+                            c0 = (K // 4) * half + 256 * (2 * j + tt) + 128 * u
                         nc.tensor.transpose(bank[:, tt, u, :], ww[:, c0:c0 + P], ident_f[:])
                 banks[j] = bank
             grp = gpool.tile([P, 8 * N_TILE], BF16, tag="grp", name="grp", align_bytes=64)
             grps[h] = grp
             gw = grp[:].bitcast(F32).rearrange("p (n u) -> p n u", u=2)
-            for i, j in enumerate(BANK_ORDER):
+            for i, j in enumerate(BANK_ORDER if h < 2 else range(4)):
                 if i == 1 and between:
                     between()
                 dst = gw[:, 256 * j:256 * (j + 1), :].rearrange("p (tt o) u -> p tt o u", tt=2)
@@ -262,49 +274,49 @@ def tile_kanlayer_w_kernel(tc, x, base_weight_words, base_weight_scales, spline_
                                       in_=grps[h][:, 4 * c * wq:4 * (c + 1) * wq])
             cods[h] = (codes, scl)
 
+        def mx(out, g, codes, scl, cj, start, stop):
+            nc.tensor.matmul_mx(
+                out=out, lhsT=bcodes[:, g, :].bitcast(FP8X4), lhsT_scale=bscl[:, g, :],
+                rhs=codes[:, cj].bitcast(FP8X4), rhs_scale=scl[:, cj], start=start, stop=stop)
+
+        def mx_base(out, g, cols):
+            nc.tensor.matmul_mx(
+                out=out, lhsT=xcodes[:, g, :].bitcast(FP8X4), lhsT_scale=xscl[:, g, :],
+                rhs=bw[:, g, cols].bitcast(FP8X4), rhs_scale=planes[:, g, cols], start=False, stop=False)
+
         def passes(h):
             n, half = h // 2, h % 2
             kc, oq = units[n]
-            opens = half == 0 and (kc == 0 or kc - 1 in CLOSES[oq])
-            closes = half == 1 and kc in CLOSES[oq]
-            cols = slice(oq * N_TILE, (oq + 1) * N_TILE)
-            if opens:
-                acc_tag[oq] = free_banks.pop(0)
-                acc_tile = psum.tile([P, N_TILE], F32, tag=acc_tag[oq], name="acc")
-                acc[oq] = acc_tile
             codes, scl = cods[h]
-            for j in range(2):
-                g = kc * PASSES_U + 2 * half + j
-                cj = slice(j * N_TILE, (j + 1) * N_TILE)
-                nc.tensor.matmul_mx(
-                    out=acc[oq][:],
-                    lhsT=bcodes[:, g, :].bitcast(FP8X4), lhsT_scale=bscl[:, g, :],
-                    rhs=codes[:, cj].bitcast(FP8X4), rhs_scale=scl[:, cj],
-                    start=(opens and j == 0), stop=(closes and j == 1),
-                )
-                if j == 0 and kc == BASE_KC:
-                    nc.tensor.matmul_mx(
-                        out=acc[oq][:],
-                        lhsT=xcodes[:, half, :].bitcast(FP8X4), lhsT_scale=xscl[:, half, :],
-                        rhs=bw[:, half, cols].bitcast(FP8X4), rhs_scale=planes[:, half, cols],
-                        start=False, stop=False,
-                    )
-            if closes:
-                closed.append((oq, kc))
+            if n < n_tiles:
+                width, c0, key = N_TILE, oq * N_TILE, oq
+                g0 = kc * PASSES_U + 2 * half
+                base = half if kc == BASE_KC else None
+            else:
+                width, c0, key = P, (N_OQ - 1) * N_TILE + P * oq, N_OQ + oq
+                g0 = 8 * half
+                base = half
+            cols = slice(c0, c0 + width)
+            if g0 == 0:
+                acc_tag[key] = free_banks.pop(0)
+                acc_tile = psum.tile([P, N_TILE], F32, tag=acc_tag[key], name="acc")
+                acc[key] = acc_tile
+            out_ap = acc[key][:, 0:width]
+            n_pass = 2 * N_TILE // width
+            for j in range(n_pass):
+                g = g0 + j
+                mx(out_ap, g, codes, scl, slice(j * width, (j + 1) * width), g == 0, g == K // 512 - 1)
+                if j == 0 and base is not None:
+                    mx_base(out_ap, base, cols)
+            if g0 + n_pass == K // 512:
+                closed.append((key, cols))
 
         def empty_sums():
             while closed:
-                oq, kc = closed.pop(0)
-                cols = slice(oq * N_TILE, (oq + 1) * N_TILE)
-                if kc != CLOSES[oq][0]:
-                    nc.vector.tensor_tensor(out=sums[:, cols], in0=acc[oq][:], in1=sums[:, cols], op=ALU.add)
-                elif kc == N_KC - 1:
-                    nc.vector.tensor_copy(out=sums[:, cols], in_=acc[oq][:])
-                else:
-                    nc.scalar.copy(out=sums[:, cols], in_=acc[oq][:])
-                if kc == N_KC - 1:
-                    nc.sync.dma_start(out=out[:, cols], in_=sums[:, cols])
-                free_banks.append(acc_tag[oq])
+                key, cols = closed.pop(0)
+                nc.vector.tensor_copy(out=sums[:, cols], in_=acc[key][:, 0:cols.stop - cols.start])
+                nc.sync.dma_start(out=out[:, cols], in_=sums[:, cols])
+                free_banks.append(acc_tag[key])
 
         st_y(0)
         st_r0(0)

@@ -63,11 +63,10 @@ def tile_kanlayer_w_kernel(tc, x, base_weight_words, base_weight_scales, spline_
             wtiles[n] = wraw
             if kc is None:
                 o0 = (N_OQ - 1) * N_TILE + P * oq
-                k_pieces = 2 if n == len(units) - 1 else 1
+                cuts = (0, K // 2, 3 * K // 4, K) if n == len(units) - 1 else (0, K)
                 row = wraw[:].rearrange("p t k -> p (t k)")
-                for c in range(k_pieces):
-                    ks = slice(c * K // k_pieces, (c + 1) * K // k_pieces)
-                    nc.sync.dma_start(out=row[:, ks], in_=w2[o0:o0 + P, ks])
+                for k0, k1 in zip(cuts, cuts[1:]):
+                    nc.sync.dma_start(out=row[:, k0:k1], in_=w2[o0:o0 + P, k0:k1])
                 return
             src = w2[oq * N_TILE:(oq + 1) * N_TILE, kc * KC:(kc + 1) * KC].rearrange("(t p) k -> p t k", p=P)
             k_pieces = 2 if n < 2 else 1
@@ -135,9 +134,13 @@ def tile_kanlayer_w_kernel(tc, x, base_weight_words, base_weight_scales, spline_
                 in1=shift[:].unsqueeze(1).to_broadcast([P, F, 2]), op0=ALU.mult, op1=ALU.add)
             bt[c] = {"y": y}
 
-        def st_r0(c):
-            z = b1pool.tile([P, 2 * F], F32, tag="z", name="z")
+        def st_z(c):
+            z = bpool.tile([P, 2 * F], F32, tag="z", name="z")
             nc.scalar.activation(out=z[:], in_=bt[c]["y"][:].rearrange("p i v -> p (i v)"), func=ACT.Abs)
+            bt[c]["z"] = z
+
+        def st_r0(c):
+            z = bt[c]["z"]
             r = bpool.tile([P, 2, 2 * F], F32, tag="r", name="r")
             nc.scalar.activation(out=r[:, 0], in_=z[:], func=ACT.Abs, bias=minus2[:])
             bt[c]["r"] = r
@@ -319,8 +322,10 @@ def tile_kanlayer_w_kernel(tc, x, base_weight_words, base_weight_scales, spline_
                 free_banks.append(acc_tag[key])
 
         st_y(0)
-        st_r0(0)
+        st_z(0)
         st_y(1)
+        st_z(1)
+        st_r0(0)
         st_m(0)
         st_r2(0)
 
@@ -333,8 +338,8 @@ def tile_kanlayer_w_kernel(tc, x, base_weight_words, base_weight_scales, spline_
                 next_pass[0] += 1
 
         plan = {}
-        for c, steps in ((1, (None, 1, None, None, 2, None, 4, 5, 6, 7, 8, 9, 9)), (2, (5, 6, 7, 7, 8, 9, 10, 11, 12, 13, 14, 15, 15)), (3, (11, 12, 13, 13, 14, 15, 16, 17, 18, 19, 20, 21, 21))):
-            for (at, fn), h in zip((("v", st_y), ("s", st_r0), ("v", st_r2), ("v", st_m), ("s", st_w), ("v", st_f1), ("v", st_g), ("v", st_b), ("v", st_s), ("v", st_n), ("t", st_t), ("e", st_e), ("v", st_q)), steps):
+        for c, steps in ((1, (None, None, 1, None, None, 2, None, 4, 5, 6, 7, 8, 9, 9)), (2, (5, 6, 7, 7, 7, 8, 9, 10, 11, 12, 13, 14, 15, 15)), (3, (11, 12, 13, 13, 13, 14, 15, 16, 17, 18, 19, 20, 21, 21))):
+            for (at, fn), h in zip((("v", st_y), ("s", st_z), ("s", st_r0), ("v", st_r2), ("v", st_m), ("s", st_w), ("v", st_f1), ("v", st_g), ("v", st_b), ("v", st_s), ("v", st_n), ("t", st_t), ("e", st_e), ("v", st_q)), steps):
                 if h is not None:
                     plan.setdefault((h, at), []).append((fn, c))
 

@@ -128,7 +128,7 @@ def tile_kanlayer_w_kernel(tc, x, base_weight_words, base_weight_scales, spline_
         bt = {}
 
         def st_y(c):
-            y = bpool.tile([P, F, 2], F32, tag="y", name="y")
+            y = bpool.tile([P, F, 2], F32, tag="y", name="y", bufs=3)
             nc.vector.scalar_tensor_tensor(
                 out=y[:], in0=x_sb[:, c * F:(c + 1) * F].unsqueeze(2).to_broadcast([P, F, 2]), scalar=2.5,
                 in1=shift[:].unsqueeze(1).to_broadcast([P, F, 2]), op0=ALU.mult, op1=ALU.add)
@@ -327,7 +327,10 @@ def tile_kanlayer_w_kernel(tc, x, base_weight_words, base_weight_scales, spline_
         st_z(1)
         st_r0(0)
         st_m(0)
+        st_y(2)
         st_r2(0)
+        st_w(0)
+        st_m(1)
 
         NH = 2 * len(units)
         next_pass = [0]
@@ -338,7 +341,7 @@ def tile_kanlayer_w_kernel(tc, x, base_weight_words, base_weight_scales, spline_
                 next_pass[0] += 1
 
         plan = {}
-        for c, steps in ((1, (None, None, 1, None, None, 2, None, 4, 5, 6, 7, 8, 9, 9)), (2, (5, 6, 7, 7, 7, 8, 9, 10, 11, 12, 13, 14, 15, 15)), (3, (11, 12, 13, 13, 13, 14, 15, 16, 17, 18, 19, 20, 21, 21))):
+        for c, steps in ((1, (None, None, 1, None, None, 2, None, 4, 5, 6, 7, 8, 9, 9)), (2, (None, 6, 7, 8, 7, 8, 9, 10, 11, 12, 13, 14, 15, 15)), (3, (11, 12, 13, 14, 13, 14, 15, 16, 17, 18, 19, 20, 21, 21))):
             for (at, fn), h in zip((("v", st_y), ("s", st_z), ("s", st_r0), ("v", st_r2), ("v", st_m), ("s", st_w), ("v", st_f1), ("v", st_g), ("v", st_b), ("v", st_s), ("v", st_n), ("t", st_t), ("e", st_e), ("v", st_q)), steps):
                 if h is not None:
                     plan.setdefault((h, at), []).append((fn, c))
@@ -355,7 +358,7 @@ def tile_kanlayer_w_kernel(tc, x, base_weight_words, base_weight_scales, spline_
             run(h, "e")
             flush = list(closed)
             if h == 0:
-                transposes_and_copies(0, (), lambda: st_w(0))
+                transposes_and_copies(0, ())
                 st_f1(0)
                 st_g(0)
             elif h < NH:
@@ -372,7 +375,6 @@ def tile_kanlayer_w_kernel(tc, x, base_weight_words, base_weight_scales, spline_
                 quantise(h - 1)
             if h == 1:
                 st_b(0)
-                st_m(1)
             if h == 2:
                 st_s(0)
                 st_r2(1)

@@ -63,14 +63,14 @@ def tile_kanlayer_w_kernel(tc, x, base_weight_words, base_weight_scales, spline_
             wtiles[n] = wraw
             if kc is None:
                 o0 = (N_OQ - 1) * N_TILE + P * oq
-                cuts = (0, K // 2, 3 * K // 4, K) if n == len(units) - 1 else (0, K)
+                cuts = (0, K // 2, 3 * K // 4, 7 * K // 8, K) if n == len(units) - 1 else (0, K)
                 row = wraw[:].rearrange("p t k -> p (t k)")
                 for k0, k1 in zip(cuts, cuts[1:]):
                     nc.sync.dma_start(out=row[:, k0:k1], in_=w2[o0:o0 + P, k0:k1])
                 return
             src = w2[oq * N_TILE:(oq + 1) * N_TILE, kc * KC:(kc + 1) * KC].rearrange("(t p) k -> p t k", p=P)
-            k_pieces = 2 if n < 2 else 1
-            t_pieces = 2 if n == 0 else 1
+            k_pieces = 1
+            t_pieces = 2 if n < 2 else 1
             kp, tp = KC // k_pieces, 4 // t_pieces
             for c in range(k_pieces):
                 for d in range(t_pieces):
@@ -112,6 +112,7 @@ def tile_kanlayer_w_kernel(tc, x, base_weight_words, base_weight_scales, spline_
         acc = {}
         acc_tag = {}
         closed = []
+        ready_cols = []
 
         def load_base():
             for q in range(4):
@@ -270,11 +271,10 @@ def tile_kanlayer_w_kernel(tc, x, base_weight_words, base_weight_scales, spline_
         def quantise(h):
             codes = cpool.tile([P, 2 * N_TILE], U32, tag="codes", name="codes", align_bytes=64)
             scl = cpool.tile([P, 2 * N_TILE], U8, tag="scl", name="scl", align_bytes=64)
-            n_cuts = 2 if h == 2 * len(units) - 1 else 1
-            wq = 2 * N_TILE // n_cuts
-            for c in range(n_cuts):
-                nc.vector.quantize_mx(out=codes[:, c * wq:(c + 1) * wq].bitcast(FP8X4), scales=scl[:, c * wq:(c + 1) * wq],
-                                      in_=grps[h][:, 4 * c * wq:4 * (c + 1) * wq])
+            words = 2 * N_TILE
+            cuts = (0, words // 2, 3 * words // 4, words) if h == 2 * len(units) - 1 else (0, words)
+            for c0, c1 in zip(cuts, cuts[1:]):
+                nc.vector.quantize_mx(out=codes[:, c0:c1].bitcast(FP8X4), scales=scl[:, c0:c1], in_=grps[h][:, 4 * c0:4 * c1])
             cods[h] = (codes, scl)
 
         def mx(out, g, codes, scl, cj, start, stop):
@@ -318,8 +318,20 @@ def tile_kanlayer_w_kernel(tc, x, base_weight_words, base_weight_scales, spline_
             while closed:
                 key, cols = closed.pop(0)
                 nc.vector.tensor_copy(out=sums[:, cols], in_=acc[key][:, 0:cols.stop - cols.start])
-                nc.sync.dma_start(out=out[:, cols], in_=sums[:, cols])
+                ready_cols.append(cols)
                 free_banks.append(acc_tag[key])
+
+        def store_sums():
+            while ready_cols:
+                start, stop = ready_cols[0].start, ready_cols[0].stop
+                if stop < O - N_TILE and (stop - start) % N_TILE:
+                    run = [c for c in ready_cols if c.start // N_TILE == start // N_TILE]
+                    if run[-1].stop % N_TILE:
+                        break
+                    stop = run[-1].stop
+                while ready_cols and ready_cols[0].start < stop:
+                    ready_cols.pop(0)
+                nc.sync.dma_start(out=out[:, start:stop], in_=sums[:, start:stop])
 
         st_y(0)
         st_z(0)
@@ -387,4 +399,6 @@ def tile_kanlayer_w_kernel(tc, x, base_weight_words, base_weight_scales, spline_
                 x_quantise()
             if flush or h >= NH:
                 empty_sums()
+            if h // 2 + 3 >= len(units) - 1:
+                store_sums()
             run(h, "v")

from contextlib import ExitStack

from concourse import mybir
from concourse.masks import make_identity

F32 = mybir.dt.float32
BF16 = mybir.dt.bfloat16
U32 = mybir.dt.uint32
U8 = mybir.dt.uint8
I32 = mybir.dt.int32
FP8X4 = mybir.dt.float8_e4m3fn_x4
ACT = mybir.ActivationFunctionType
ALU = mybir.AluOpType
AX = mybir.AxisListType

P = 128
B, I, O, L = 128, 1024, 2048, 8
K = I * L
FLOPS = 2 * B * (I + K) * O
N_TILE = 512
KC = 2048
PASSES_U = KC // 512
N_OQ = O // N_TILE
N_KC = K // KC
F = KC // L
BANK_ORDER = (0, 2, 1, 3)
BASE_KC = 2
LAG = 4
LAG0 = 5
GROUP = 1


def tile_kanlayer_w_kernel(tc, x, base_weight_words, base_weight_scales, spline_weight, out):
    nc = tc.nc
    w2 = spline_weight.rearrange("o i l -> o (i l)")
    with ExitStack() as ctx:
        const = ctx.enter_context(tc.tile_pool(name="const", bufs=1))
        wpool = ctx.enter_context(tc.tile_pool(name="wraw", bufs=4))
        gpool = ctx.enter_context(tc.tile_pool(name="grp", bufs=4))
        cpool = ctx.enter_context(tc.tile_pool(name="codes", bufs=8))
        bpool = ctx.enter_context(tc.tile_pool(name="basis", bufs=2))
        b1pool = ctx.enter_context(tc.tile_pool(name="basis1", bufs=1))
        psum = ctx.enter_context(tc.psum_pool(name="psum", bufs=1))
        ctx.enter_context(tc.manual_schedule())

        x_sb = const.tile([P, I], BF16, align_bytes=64)
        nc.sync.dma_start(out=x_sb[:], in_=x)
        units = [(kc, oq) for kc in range(N_KC) for oq in range(N_OQ - 1)]
        n_tiles = len(units)
        units += [(None, t) for t in range(4)]
        free_banks = ["bank%d" % i for i in range(8)]

        def transposes_bank():
            tag = free_banks.pop(0)
            free_banks.append(tag)
            bank = psum.tile([P, 2, 2, P], F32, tag=tag, name="bank")
            return bank
        wtiles = {}

        def load_unit(n):
            kc, oq = units[n]
            wraw = wpool.tile([P, 4, KC], BF16, tag="wraw", name="wraw")
            wtiles[n] = wraw
            if kc is None:
                o0 = (N_OQ - 1) * N_TILE + P * oq
                cuts = (0, K // 2, 3 * K // 4, 7 * K // 8, K) if n == len(units) - 1 else (0, K)
                row = wraw[:].rearrange("p t k -> p (t k)")
                for k0, k1 in zip(cuts, cuts[1:]):
                    nc.sync.dma_start(out=row[:, k0:k1], in_=w2[o0:o0 + P, k0:k1])
                return
            src = w2[oq * N_TILE:(oq + 1) * N_TILE, kc * KC:(kc + 1) * KC].rearrange("(t p) k -> p t k", p=P)
            k_pieces = 1
            t_pieces = 2 if n < 2 else 1
            kp, tp = KC // k_pieces, 4 // t_pieces
            for c in range(k_pieces):
                for d in range(t_pieces):
                    part = (slice(None), slice(d * tp, (d + 1) * tp), slice(c * kp, (c + 1) * kp))
                    nc.sync.dma_start(out=wraw[part], in_=src[part])
            wtiles[n] = wraw

        for n in range(3):
            load_unit(n)

        warm = const.tile([P, 2], F32)
        nc.vector.memset(warm[:, 0:1], 0.0)
        nc.scalar.activation(out=warm[:, 1:2], in_=warm[:, 0:1], func=ACT.Abs)
        shift = const.tile([P, 2], F32)
        for v in range(2):
            nc.vector.memset(shift[:, v:v + 1], -0.5 - v)
        minus2 = const.tile([P, 1], F32)
        nc.vector.memset(minus2[:], -2.0)

        ident_f = const.tile([P, P], F32)
        make_identity(nc, ident_f[:])
        planes = const.tile([P, 2, O], U8, align_bytes=64)
        nc.vector.memset(planes[:].rearrange("p g n -> p (g n)").bitcast(I32), 0)
        sgn = const.tile([P, 1], F32)
        lrow = const.tile([P, 32, 4], F32)
        for q in range(4):
            nc.vector.memset(lrow[:, :, q], 4.0 * (q // 2) - 2.0)
        lsel = const.tile([P, P], F32)
        nc.vector.tensor_tensor(out=lsel[:], in0=ident_f[:], in1=lrow[:].rearrange("p a r -> p (a r)"), op=ALU.mult)
        nc.vector.tensor_reduce(out=sgn[:], in_=lsel[:], axis=AX.X, op=ALU.add)

        bcodes = const.tile([P, K // 512, B], U32, align_bytes=64)
        bscl = const.tile([P, K // 512, B], U8, align_bytes=64)
        xcodes = const.tile([P, 2, B], U32, align_bytes=64)
        xscl = const.tile([P, 2, B], U8, align_bytes=64)
        bw = const.tile([P, 2, O], U32, align_bytes=64)
        xg = const.tile([P, 2 * B * 4], BF16, align_bytes=64)
        sums = const.tile([P, O], F32, align_bytes=64)
        acc = {}
        acc_tag = {}
        closed = []
        ready_cols = []

        def load_base():
            for q in range(4):
                nc.sync.dma_start(
                    out=planes[32 * q:32 * q + 4, :, :].bitcast(I32),
                    in_=base_weight_scales[:, 4 * q:4 * q + 4, :].rearrange("g r n -> r g n").bitcast(I32),
                )
            for g in range(2):
                nc.sync.dma_start(
                    out=bw[:, g, :].bitcast(I32),
                    in_=base_weight_words[g].rearrange("p n t -> p (n t)").bitcast(I32),
                )

        bt = {}

        def st_y(c):
            y = bpool.tile([P, F, 2], F32, tag="y", name="y", bufs=3)
            nc.vector.scalar_tensor_tensor(
                out=y[:], in0=x_sb[:, c * F:(c + 1) * F].unsqueeze(2).to_broadcast([P, F, 2]), scalar=2.5,
                in1=shift[:].unsqueeze(1).to_broadcast([P, F, 2]), op0=ALU.mult, op1=ALU.add)
            bt[c] = {"y": y}

        def st_z(c):
            z = bpool.tile([P, 2 * F], F32, tag="z", name="z")
            nc.scalar.activation(out=z[:], in_=bt[c]["y"][:].rearrange("p i v -> p (i v)"), func=ACT.Abs)
            bt[c]["z"] = z

        def st_r0(c):
            z = bt[c]["z"]
            r = bpool.tile([P, 2, 2 * F], F32, tag="r", name="r")
            nc.scalar.activation(out=r[:, 0], in_=z[:], func=ACT.Abs, bias=minus2[:])
            bt[c]["r"] = r

        def st_r2(c):
            r = bt[c]["r"]
            nc.vector.tensor_scalar(out=r[:, 1], in0=r[:, 0], scalar1=-1.0, scalar2=2.0, op0=ALU.mult, op1=ALU.add)

        def st_m(c):
            m = bpool.tile([P, 2, 2 * F], BF16, tag="m", name="m")
            for h in range(2):
                nc.vector.tensor_scalar(out=m[:, h], in0=bt[c]["y"][:].rearrange("p i v -> p (i v)"),
                                        scalar1=2.0 * h - 2.0, scalar2=0.5, op0=ALU.is_ge, op1=ALU.subtract)
            bt[c]["m"] = m

        def st_w(c):
            w = bpool.tile([P, 2, 2 * F], F32, tag="w", name="w")
            r0 = bt[c]["r"][:, 0]
            nc.scalar.activation(out=w[:, 0], in_=r0, func=ACT.Square)
            nc.scalar.activation(out=w[:, 1], in_=r0, func=ACT.Square, bias=minus2[:])
            bt[c]["w"] = w

        def st_f1(c):
            f1 = b1pool.tile([P, 2, 2 * F], F32, tag="f1", name="f1")
            nc.vector.scalar_tensor_tensor(out=f1[:], in0=bt[c]["w"][:], scalar=1.0 / 6.0, in1=bt[c]["r"][:],
                                           op0=ALU.mult, op1=ALU.mult)
            bt[c]["f1"] = f1

        def st_g(c):
            g = b1pool.tile([P, 2, 2 * F], F32, tag="g", name="g")
            for h in range(2):
                nc.vector.scalar_tensor_tensor(out=g[:, h], in0=bt[c]["w"][:, 1 - h], scalar=-0.5,
                                               in1=bt[c]["r"][:, h], op0=ALU.mult, op1=ALU.mult)
            bt[c]["g"] = g

        def st_b(c):
            b = bpool.tile([P, 2, 2 * F], BF16, tag="b", name="b")
            nc.vector.scalar_tensor_tensor(out=b[:], in0=bt[c]["g"][:], scalar=2.0 / 3.0, in1=bt[c]["f1"][:],
                                           op0=ALU.add, op1=ALU.min)
            bt[c]["b"] = b

        def st_s(c):
            s = b1pool.tile([P, F, 2, 2], BF16, tag="s", name="s")
            nc.vector.tensor_tensor(out=s[:], in0=bt[c]["b"][:].rearrange("p h (i v) -> p i h v", v=2),
                                    in1=bt[c]["m"][:].rearrange("p h (i v) -> p i h v", v=2), op=ALU.mult)
            bt[c]["s"] = s

        def st_n(c):
            nat = b1pool.tile([P, F, 2, 4], BF16, tag="nat", name="nat", align_bytes=64)
            nc.vector.tensor_copy(
                out=nat[:],
                in_=bt[c]["s"][:].rearrange("p i h v -> p i (h v)").unsqueeze(2).to_broadcast([P, F, 2, 4]))
            bt[c]["nat"] = nat

        def st_t(c):
            words = bt[c]["nat"][:].rearrange("p i a q -> p (i a q)").bitcast(F32)
            bt[c]["banks"] = []
            for d in range(2):
                bank = transposes_bank()
                for g in range(2):
                    for u in range(2):
                        c0 = 512 * d + 256 * g + 128 * u
                        nc.tensor.transpose(bank[:, u, g, :], words[:, c0:c0 + P], ident_f[:])
                bt[c]["banks"].append(bank)

        def st_e(c):
            bg = b1pool.tile([P, 8 * F], BF16, tag="bg", name="bg", align_bytes=64)
            for d in range(2):
                src = bt[c]["banks"][d][:].rearrange("p u g b -> p (u g b)").bitcast(BF16)
                nc.vector.tensor_scalar(
                    out=bg[:, 1024 * d:1024 * (d + 1)].rearrange("p (n u e) -> p n u e", u=2, e=2),
                    in0=src.rearrange("p (u n e) -> p n u e", u=2, e=2),
                    scalar1=sgn[:], scalar2=0.0, op0=ALU.mult, op1=ALU.max)
            bt[c]["bg"] = bg

        def st_q(c):
            nc.vector.quantize_mx(
                out=bcodes[:, 4 * c:4 * c + 4, :].rearrange("p g b -> p (g b)").bitcast(FP8X4),
                scales=bscl[:, 4 * c:4 * c + 4, :].rearrange("p g b -> p (g b)"),
                in_=bt[c]["bg"][:],
            )

        def x_transposes():
            xw = x_sb[:].bitcast(F32)
            xt = transposes_bank()
            for g in range(2):
                for u in range(2):
                    nc.tensor.transpose(xt[:, g, u, :], xw[:, 256 * g + u:256 * (g + 1):2], ident_f[:])
            nc.scalar.copy(out=xg[:].bitcast(F32).rearrange("p (g b u) -> p g b u", g=2, u=2),
                           in_=xt[:].rearrange("p g u b -> p g b u"))

        def x_quantise():
            nc.vector.quantize_mx(out=xcodes[:].rearrange("p g b -> p (g b)").bitcast(FP8X4),
                                  scales=xscl[:].rearrange("p g b -> p (g b)"), in_=xg[:])

        grps = {}
        cods = {}

        def transposes_and_copies(h, n_vec, between=None):
            n, half = h // 2, h % 2
            ww = wtiles[n][:].rearrange("p t k -> p (t k)").bitcast(F32)
            banks = {}
            for j in (BANK_ORDER if h < 2 else range(4)):
                gl, th = 2 * half + j // 2, j % 2
                bank = transposes_bank()
                for tt in range(2):
                    for u in range(2):
                        if n < n_tiles:
                            c0 = (2 * th + tt) * (KC // 2) + 256 * gl + 128 * u
                        else:
                            c0 = (K // 4) * half + 256 * (2 * j + tt) + 128 * u
                        nc.tensor.transpose(bank[:, tt, u, :], ww[:, c0:c0 + P], ident_f[:])
                banks[j] = bank
            grp = gpool.tile([P, 8 * N_TILE], BF16, tag="grp", name="grp", align_bytes=64)
            grps[h] = grp
            gw = grp[:].bitcast(F32).rearrange("p (n u) -> p n u", u=2)
            for i, j in enumerate(BANK_ORDER if h < 2 else range(4)):
                if i == 1 and between:
                    between()
                dst = gw[:, 256 * j:256 * (j + 1), :].rearrange("p (tt o) u -> p tt o u", tt=2)
                src = banks[j][:].rearrange("p tt u o -> p tt o u")
                if j in n_vec:
                    nc.vector.tensor_copy(out=dst, in_=src)
                else:
                    nc.scalar.copy(out=dst, in_=src)

        def quantise(h):
            codes = cpool.tile([P, 2 * N_TILE], U32, tag="codes", name="codes", align_bytes=64)
            scl = cpool.tile([P, 2 * N_TILE], U8, tag="scl", name="scl", align_bytes=64)
            words = 2 * N_TILE
            cuts = (0, words // 2, 3 * words // 4, words) if h == 2 * len(units) - 1 else (0, words)
            for c0, c1 in zip(cuts, cuts[1:]):
                nc.vector.quantize_mx(out=codes[:, c0:c1].bitcast(FP8X4), scales=scl[:, c0:c1], in_=grps[h][:, 4 * c0:4 * c1])
            cods[h] = (codes, scl)

        def mx(out, g, codes, scl, cj, start, stop):
            nc.tensor.matmul_mx(
                out=out, lhsT=bcodes[:, g, :].bitcast(FP8X4), lhsT_scale=bscl[:, g, :],
                rhs=codes[:, cj].bitcast(FP8X4), rhs_scale=scl[:, cj], start=start, stop=stop)

        def mx_base(out, g, cols):
            nc.tensor.matmul_mx(
                out=out, lhsT=xcodes[:, g, :].bitcast(FP8X4), lhsT_scale=xscl[:, g, :],
                rhs=bw[:, g, cols].bitcast(FP8X4), rhs_scale=planes[:, g, cols], start=False, stop=False)

        def passes(h):
            n, half = h // 2, h % 2
            kc, oq = units[n]
            codes, scl = cods[h]
            if n < n_tiles:
                width, c0, key = N_TILE, oq * N_TILE, oq
                g0 = kc * PASSES_U + 2 * half
                base = half if kc == BASE_KC else None
            else:
                width, c0, key = P, (N_OQ - 1) * N_TILE + P * oq, N_OQ + oq
                g0 = 8 * half
                base = half
            cols = slice(c0, c0 + width)
            if g0 == 0:
                acc_tag[key] = free_banks.pop(0)
                acc_tile = psum.tile([P, N_TILE], F32, tag=acc_tag[key], name="acc")
                acc[key] = acc_tile
            out_ap = acc[key][:, 0:width]
            n_pass = 2 * N_TILE // width
            for j in range(n_pass):
                g = g0 + j
                mx(out_ap, g, codes, scl, slice(j * width, (j + 1) * width), g == 0, g == K // 512 - 1)
                if j == 0 and base is not None:
                    mx_base(out_ap, base, cols)
            if g0 + n_pass == K // 512:
                closed.append((key, cols))

        def empty_sums():
            while closed:
                key, cols = closed.pop(0)
                nc.vector.tensor_copy(out=sums[:, cols], in_=acc[key][:, 0:cols.stop - cols.start])
                ready_cols.append(cols)
                free_banks.append(acc_tag[key])

        def store_sums():
            while ready_cols:
                start, stop = ready_cols[0].start, ready_cols[0].stop
                if stop < O - N_TILE and (stop - start) % N_TILE:
                    run = [c for c in ready_cols if c.start // N_TILE == start // N_TILE]
                    if run[-1].stop % N_TILE:
                        break
                    stop = run[-1].stop
                while ready_cols and ready_cols[0].start < stop:
                    ready_cols.pop(0)
                nc.sync.dma_start(out=out[:, start:stop], in_=sums[:, start:stop])

        st_y(0)
        st_z(0)
        st_y(1)
        st_z(1)
        st_r0(0)
        st_m(0)
        st_y(2)
        st_r2(0)
        st_w(0)
        st_m(1)

        NH = 2 * len(units)
        next_pass = [0]

        def passes_up_to(last):
            while next_pass[0] <= last:
                passes(next_pass[0])
                next_pass[0] += 1

        plan = {}
        for c, steps in ((1, (None, None, 1, None, None, 2, None, 4, 5, 6, 7, 8, 9, 9)), (2, (None, 6, 7, 8, 7, 8, 9, 10, 11, 12, 13, 14, 15, 15)), (3, (11, 12, 13, 14, 13, 14, 15, 16, 17, 18, 19, 20, 21, 21))):
            for (at, fn), h in zip((("v", st_y), ("s", st_z), ("s", st_r0), ("v", st_r2), ("v", st_m), ("s", st_w), ("v", st_f1), ("v", st_g), ("v", st_b), ("v", st_s), ("v", st_n), ("t", st_t), ("e", st_e), ("v", st_q)), steps):
                if h is not None:
                    plan.setdefault((h, at), []).append((fn, c))

        def run(h, at):
            for fn, c in plan.get((h, at), ()):
                fn(c)

        for h in range(NH + LAG):
            if h % 2 == 0 and h // 2 + 3 < len(units):
                load_unit(h // 2 + 3)
                if h == 8:
                    load_base()
            run(h, "e")
            flush = list(closed)
            if h == 0:
                transposes_and_copies(0, ())
                st_f1(0)
                st_g(0)
            elif h < NH:
                transposes_and_copies(h, (0,) if h > 24 else ())
            if h == 3:
                st_t(0)
            if h == 7:
                x_transposes()
            run(h, "s")
            if h >= LAG0 and (h < 24 or h % 2 == 0 or h >= NH):
                passes_up_to(min(h - LAG, 2 * (h - LAG0) + 1) if h < NH else h - LAG)
            run(h, "t")
            if 1 <= h <= NH:
                quantise(h - 1)
            if h == 1:
                st_b(0)
            if h == 2:
                st_s(0)
                st_r2(1)
                st_n(0)
            if h == 3:
                st_e(0)
                st_f1(1)
                st_q(0)
            if h == 7 + 1:
                x_quantise()
            if flush or h >= NH:
                empty_sums()
            if h // 2 + 3 >= len(units) - 1:
                store_sums()
            run(h, "v")
